import numpy as np
import ml_dtypes


def mxq(x, axis, fmt="e4m3"):
    dtype, down = {"e4m3": (ml_dtypes.float8_e4m3fn, 7), "e5m2": (ml_dtypes.float8_e5m2, 14)}[fmt]
    v = np.moveaxis(np.asarray(x, np.float32).astype(ml_dtypes.bfloat16).astype(np.float64), axis, -1)
    blocks = v.reshape(v.shape[:-1] + (-1, 32))
    amax = np.abs(blocks).max(-1, keepdims=True)
    byte = np.maximum(np.where(amax > 0, np.frexp(amax)[1] - 1 + 127, 0) - down, 1)
    scale = np.exp2(byte - 127.0)
    codes = (blocks / scale).astype(np.float32).astype(dtype).astype(np.float64)
    return np.moveaxis((codes * scale).reshape(v.shape), -1, axis)


WIDE = False


def mx_kscale(k):
    if not WIDE:
        return np.ones(k)
    levels = np.array([10, -10, 5, -5, 0])
    a = np.random.permutation(np.resize(levels, k // 512 * 4)).reshape(k // 512, 4)
    idx = np.arange(k)
    return np.exp2(a[idx // 512, idx % 128 // 32])


BF16 = ml_dtypes.bfloat16


def bf(x):
    return np.asarray(x, np.float32).astype(BF16)


def f64(x):
    return np.asarray(x).astype(np.float64)


E2M1 = np.array([0.0, 0.5, 1.0, 1.5, 2.0, 3.0, 4.0, 6.0, -0.0, -0.5, -1.0, -1.5, -2.0, -3.0, -4.0, -6.0])


def pack_weight(w, fmt):
    k, n = w.shape
    w = f64(bf(w)).reshape(k // 32, 32, n)
    amax = np.abs(w).max(1)
    if fmt == "e4m3":
        byte = np.frexp(amax)[1] - 1 + 127 - 7
    else:
        mant, ex = np.frexp(amax / 6.0)
        byte = np.where(mant > 0.5, ex, ex - 1) + 127
    byte = np.clip(np.where(amax > 0, byte, 1), 1, 254)
    scaled = (w * np.exp2(127.0 - byte)[:, None, :]).reshape(k, n).astype(np.float32)
    by_word = np.ascontiguousarray(scaled.reshape(k // 512, 128, 4, n).transpose(0, 1, 3, 2))
    if fmt == "e4m3":
        words = by_word.astype(ml_dtypes.float8_e4m3fn).view(np.uint8)
    else:
        c = by_word.astype(ml_dtypes.float4_e2m1fn).view(np.uint8) & 0xF
        words = c[..., 0::2] | (c[..., 1::2] << 4)
    return np.ascontiguousarray(words), np.ascontiguousarray(byte.astype(np.uint8).reshape(k // 512, 16, n))


def unpack_weight(words, scales, fmt):
    g, p, n, _ = words.shape
    if fmt == "e4m3":
        vals = np.ascontiguousarray(words).view(ml_dtypes.float8_e4m3fn).astype(np.float64)
    else:
        nib = np.empty((g, p, n, 4), np.uint8)
        nib[..., 0::2] = words & 0xF
        nib[..., 1::2] = words >> 4
        vals = E2M1[nib]
    vals = vals * np.repeat(np.exp2(scales.astype(np.float64) - 127.0), 8, axis=1)[..., None]
    return vals.transpose(0, 1, 3, 2).reshape(g * 512, n)


B, N, M, H, O = 24, 16, 16, 1024, 1024


def rotary(x):
    S, F = x.shape[1], x.shape[2]
    pos = np.arange(S, dtype=np.float64)[:, None]
    inv_freq = np.power(10000.0, -2.0 * np.arange(F // 2, dtype=np.float64) / F)
    ang = pos * inv_freq
    cos = np.repeat(np.cos(ang), 2, axis=-1)
    sin = np.repeat(np.sin(ang), 2, axis=-1)
    x_rot = np.stack([-x[..., 1::2], x[..., ::2]], axis=-1).reshape(x.shape)
    return x * cos + x_rot * sin


def setup_inputs():
    s = np.repeat(mx_kscale(H)[::2], 2)
    t = np.repeat(mx_kscale(H)[::2], 2)
    review = bf(np.random.standard_normal((B, N, H)) * s)
    reply = bf(np.random.standard_normal((B, M, H)) * t)
    w = np.random.standard_normal((O, 2 * H)) * 0.7 / np.sqrt(H) / np.concatenate([s, t])
    words, scales = pack_weight(w.T, "e4m3")
    b = bf(np.random.standard_normal(O) * 0.5)
    return {"review": review,
            "reply": reply,
            "W_words": words,
            "W_scales": scales,
            "b": b}


def reference(review, reply, W_words, W_scales, b):
    review = rotary(f64(review))
    reply = rotary(f64(reply))
    W = unpack_weight(W_words, W_scales, "e4m3")
    W_r, W_p = W[:H], W[H:]
    proj_review = mxq(review, 2, "e4m3") @ W_r
    proj_reply = mxq(reply, 2, "e4m3") @ W_p
    out = proj_review[:, :, None, :] + proj_reply[:, None, :, :] + f64(b)
    return np.maximum(out, 0.0)

@@ -1,0 +1,279 @@
+from contextlib import ExitStack
+import math
+
+import concourse.mybir as mybir
+from concourse.masks import make_identity
+
+F32 = mybir.dt.float32
+BF16 = mybir.dt.bfloat16
+I32 = mybir.dt.int32
+U8 = mybir.dt.uint8
+FP8X4 = mybir.dt.float8_e4m3fn_x4
+ALU = mybir.AluOpType
+ACT = mybir.ActivationFunctionType
+
+P = 128
+BATCH = 24
+POSITIONS = 16
+FEATURES = 1024
+PAIRS = FEATURES // 2
+OUT = 1024
+PACK = 4
+K_PASS = P * PACK
+PASSES = FEATURES // K_PASS
+N_TILE = 512
+HALVES = OUT // N_TILE
+J = P // POSITIONS
+GROUPS = BATCH // J
+NQ, NR = 8, 2
+MQ, MR = 2, 8
+STEP_MR = 2
+ROPE_BASE = 10000.0
+WRAPPED = 128
+
+FLOPS = 2 * 2 * BATCH * POSITIONS * FEATURES * OUT
+
+
+def tile_positionwisedtableencoder_kernel(tc, review, reply, W_words, W_scales, b, out):
+    nc = tc.nc
+    with ExitStack() as ctx:
+        const = ctx.enter_context(tc.tile_pool(name="const", bufs=1))
+        inputs = ctx.enter_context(tc.tile_pool(name="inputs", bufs=1))
+        rotated = ctx.enter_context(tc.tile_pool(name="rotated", bufs=1))
+        work = ctx.enter_context(tc.tile_pool(name="work", bufs=2))
+        packed = ctx.enter_context(tc.tile_pool(name="packed", bufs=2))
+        stages = ctx.enter_context(tc.tile_pool(name="stages", bufs=4))
+        psum_t = ctx.enter_context(tc.psum_pool(name="psum_t", bufs=2))
+        psum_acc = ctx.enter_context(tc.psum_pool(name="psum_acc", bufs=6))
+
+        review_rows = review.rearrange("(g j) n h -> g (j n) h", j=J)
+        reply_rows = reply.rearrange("(g j) m h -> g (j m) h", j=J)
+        x_review = [inputs.tile([P, FEATURES], BF16, name="x_review%d" % g) for g in range(GROUPS)]
+        x_reply = [inputs.tile([P, FEATURES], BF16, name="x_reply%d" % g) for g in range(GROUPS)]
+        nc.sync.dma_start(out=x_review[0][:], in_=review_rows[0])
+        nc.sync.dma_start(out=x_reply[0][:], in_=reply_rows[0])
+
+        w_planes = const.tile([P, OUT], U8, align_bytes=64)
+        nc.vector.memset(w_planes[:].bitcast(I32), 0)
+        for quadrant in range(4):
+            nc.sync.dma_start(
+                out=w_planes[32 * quadrant : 32 * quadrant + 16, :].bitcast(I32),
+                in_=W_scales[:, 4 * quadrant : 4 * quadrant + 4, :].bitcast(I32),
+            )
+        w_codes = const.tile([P, 2 * PASSES, OUT], I32, align_bytes=64)
+        for g in range(2 * PASSES):
+            nc.sync.dma_start(
+                out=w_codes[:, g, :], in_=W_words[g].rearrange("p n t -> p (n t)").bitcast(I32)
+            )
+        for g in range(1, GROUPS):
+            nc.sync.dma_start(out=x_review[g][:], in_=review_rows[g])
+            nc.sync.dma_start(out=x_reply[g][:], in_=reply_rows[g])
+
+        row_index = const.tile([P, 1], I32)
+        nc.gpsimd.iota(row_index[:], pattern=[[0, 1]], base=0, channel_multiplier=1)
+        identity = const.tile([P, P], F32)
+        make_identity(nc, identity[:])
+        order_review = const.tile([P, P], F32)
+        nc.gpsimd.tensor_copy(
+            out=order_review[:].rearrange("p (r j q) -> p r j q", r=NR, j=J),
+            in_=identity[:].rearrange("p (j q r) -> p r j q", j=J, r=NR),
+        )
+        order_reply = const.tile([P, P], F32)
+        nc.gpsimd.tensor_copy(
+            out=order_reply[:].rearrange("p (r j q) -> p r j q", r=MR, j=J),
+            in_=identity[:].rearrange("p (j q r) -> p r j q", j=J, r=MR),
+        )
+        bias_rows = const.tile([P, OUT], BF16)
+        nc.gpsimd.memset(bias_rows[:], 0.0)
+        nc.scalar.dma_start(out=bias_rows[0:1, :], in_=b.rearrange("(one o) -> one o", one=1))
+        ones = const.tile([P, P], BF16)
+        nc.gpsimd.memset(ones[:], 1.0)
+
+        position_int = const.tile([P, 1], I32)
+        nc.vector.tensor_single_scalar(position_int[:], row_index[:], POSITIONS - 1, op=ALU.bitwise_and)
+        position = const.tile([P, 1], F32)
+        nc.vector.tensor_copy(out=position[:], in_=position_int[:])
+        frequency = const.tile([P, PAIRS], F32)
+        nc.vector.memset(frequency[:, 0:1], 1.0)
+        filled = 1
+        while filled < PAIRS:
+            nc.vector.tensor_scalar_mul(
+                out=frequency[:, filled : 2 * filled],
+                in0=frequency[:, 0:filled],
+                scalar1=ROPE_BASE ** (-filled / PAIRS),
+            )
+            filled *= 2
+        angle = const.tile([P, 2, PAIRS], F32)
+        nc.vector.tensor_scalar_mul(out=angle[:, 0, :], in0=frequency[:], scalar1=position[:, 0:1])
+        nc.vector.tensor_scalar(
+            out=angle[:, 1, :], in0=frequency[:], scalar1=position[:, 0:1], scalar2=math.pi / 2,
+            op0=ALU.mult, op1=ALU.add,
+        )
+        turns = const.tile([P, 2, WRAPPED], I32)
+        nc.vector.tensor_scalar_mul(out=turns[:], in0=angle[:, :, 0:WRAPPED], scalar1=1.0 / (2.0 * math.pi))
+        nc.vector.scalar_tensor_tensor(
+            out=angle[:, :, 0:WRAPPED], in0=turns[:], scalar=-2.0 * math.pi, in1=angle[:, :, 0:WRAPPED],
+            op0=ALU.mult, op1=ALU.add,
+        )
+        trig = const.tile([P, 2, PAIRS], F32)
+        nc.scalar.activation(
+            out=trig[:].rearrange("p t i -> p (t i)"), in_=angle[:].rearrange("p t i -> p (t i)"), func=ACT.Sin
+        )
+        sin = trig[:, 0, :]
+        cos = trig[:, 1, :]
+        minus_sin = const.tile([P, PAIRS], F32)
+        nc.vector.tensor_scalar_mul(out=minus_sin[:], in0=sin, scalar1=-1.0)
+
+        bias_all = const.tile([P, OUT], F32)
+        for h in range(HALVES):
+            cols = slice(h * N_TILE, (h + 1) * N_TILE)
+            spread = psum_acc.tile([P, N_TILE], F32, tag="acc")
+            nc.tensor.matmul(spread[:], lhsT=ones[:], rhs=bias_rows[:, cols], start=True, stop=True)
+            nc.scalar.copy(out=bias_all[:, cols], in_=spread[:])
+
+        reply_planes = const.tile([P, PASSES * MR * J * 2 * MQ], U8, align_bytes=64)
+        nc.vector.memset(reply_planes[:].bitcast(I32), 0)
+
+        def rotate(engine, x, name):
+            pairs = x[:].rearrange("p (i e) -> p i e", e=2)
+            straight = work.tile([P, PAIRS, 2], F32, tag="straight")
+            crossed = work.tile([P, 2, PAIRS], F32, tag="crossed")
+            engine.tensor_tensor(
+                out=straight[:], in0=pairs, in1=cos.unsqueeze(2).to_broadcast([P, PAIRS, 2]), op=ALU.mult
+            )
+            engine.tensor_tensor(out=crossed[:, 0, :], in0=pairs[:, :, 1], in1=minus_sin[:], op=ALU.mult)
+            engine.tensor_tensor(out=crossed[:, 1, :], in0=pairs[:, :, 0], in1=sin, op=ALU.mult)
+            y = rotated.tile([P, PAIRS, 2], BF16, name=name)
+            engine.tensor_tensor(
+                out=y[:], in0=straight[:], in1=crossed[:].rearrange("p e i -> p i e"), op=ALU.add
+            )
+            return y
+
+        def transpose_words(y, order):
+            words = y[:].rearrange("p i e -> p (i e)").bitcast(F32)
+            planes = psum_t.tile([P, PASSES * 2, P], F32, tag="planes")
+            for g in range(PASSES):
+                for u in range(2):
+                    nc.tensor.transpose(
+                        planes[:, 2 * g + u, :], words[:, 256 * g + u : 256 * (g + 1) : 2], order[:]
+                    )
+            return planes
+
+        def pack(group, y_review, y_reply):
+            planes = transpose_words(y_review, order_review)
+            grouped = work.tile([P, PASSES, P, MQ, PACK], BF16, tag="grouped_review", align_bytes=64)
+            for g in range(PASSES):
+                nc.scalar.copy(
+                    out=grouped[:, g].bitcast(F32),
+                    in_=planes[:, 2 * g : 2 * g + 2, :]
+                    .rearrange("p u c -> p c u")
+                    .unsqueeze(2)
+                    .to_broadcast([P, P, MQ, 2]),
+                )
+            review_codes = packed.tile([P, PASSES * NR * P], I32, tag="review_codes", align_bytes=64)
+            review_planes = packed.tile([P, PASSES * NR * P], U8, tag="review_planes", align_bytes=64)
+            nc.vector.quantize_mx(
+                out=review_codes[:].bitcast(FP8X4),
+                scales=review_planes[:],
+                in_=grouped[:].rearrange("p g c r t -> p (g c r t)"),
+            )
+
+            planes = transpose_words(y_reply, order_reply)
+            grouped = work.tile([P, PASSES, MR * J, 2, MQ, PACK], BF16, tag="grouped_reply", align_bytes=64)
+            for twin in range(2):
+                nc.scalar.copy(
+                    out=grouped[:, :, :, twin, :, :].bitcast(F32),
+                    in_=planes[:].rearrange("p (g u) (a q) -> p g a q u", u=2, q=MQ),
+                )
+            reply_codes = packed.tile([P, PASSES * MR * J * 2 * MQ], I32, tag="reply_codes", align_bytes=64)
+            nc.vector.quantize_mx(
+                out=reply_codes[:].bitcast(FP8X4),
+                scales=reply_planes[:],
+                in_=grouped[:].rearrange("p g a r q t -> p (g a r q t)"),
+            )
+            spread_codes = packed.tile([P, PASSES, MR, P], I32, tag="spread_codes", align_bytes=64)
+            spread_planes = packed.tile([P, PASSES, MR, P], U8, tag="spread_planes", align_bytes=64)
+            nc.vector.tensor_copy(
+                out=spread_codes[:].rearrange("p g r (j a w) -> p (g r j) a w", a=NQ // 2, w=2 * MQ),
+                in_=reply_codes[:]
+                .rearrange("p (c w) -> p c w", w=2 * MQ)
+                .unsqueeze(2)
+                .to_broadcast([P, PASSES * MR * J, NQ // 2, 2 * MQ]),
+            )
+            nc.vector.tensor_copy(
+                out=spread_planes[:].bitcast(I32).rearrange("p g r (j a) -> p (g r j) a", a=NQ // 2),
+                in_=reply_planes[:].bitcast(I32).unsqueeze(2).to_broadcast([P, PASSES * MR * J, NQ // 2]),
+            )
+
+            review_sum = packed.tile([P, NR, OUT], F32, tag="review_sum")
+            for nr in range(NR):
+                for h in range(HALVES):
+                    cols = slice(h * N_TILE, (h + 1) * N_TILE)
+                    acc = psum_acc.tile([P, N_TILE], F32, tag="acc")
+                    for g in range(PASSES):
+                        block = slice((g * NR + nr) * P, (g * NR + nr + 1) * P)
+                        nc.tensor.matmul_mx(
+                            out=acc[:],
+                            lhsT=review_codes[:, block].bitcast(FP8X4),
+                            lhsT_scale=review_planes[:, block],
+                            rhs=w_codes[:, g, cols].bitcast(FP8X4),
+                            rhs_scale=w_planes[4 * g : P, cols],
+                            start=(g == 0),
+                            stop=(g == PASSES - 1),
+                        )
+                    nc.vector.tensor_tensor(
+                        out=review_sum[:, nr, cols], in0=acc[:], in1=bias_all[:, cols], op=ALU.add
+                    )
+            return spread_codes, spread_planes, review_sum
+
+        out_rows = out.rearrange(
+            "(g j) (nq nr) (mq mr) o -> g nr (j nq) mq (mr o)", j=J, nr=NR, mq=MQ
+        )
+
+        def table(group, spread_codes, spread_planes, review_sum):
+            for first_mr in range(0, MR, STEP_MR):
+                stage = stages.tile([P, NR, STEP_MR, OUT], F32, tag="stage")
+                for s in range(STEP_MR):
+                    mr = first_mr + s
+                    for h in range(HALVES):
+                        cols = slice(h * N_TILE, (h + 1) * N_TILE)
+                        acc = psum_acc.tile([P, N_TILE], F32, tag="acc")
+                        for g in range(PASSES):
+                            nc.tensor.matmul_mx(
+                                out=acc[:],
+                                lhsT=spread_codes[:, g, mr, :].bitcast(FP8X4),
+                                lhsT_scale=spread_planes[:, g, mr, :],
+                                rhs=w_codes[:, PASSES + g, cols].bitcast(FP8X4),
+                                rhs_scale=w_planes[4 * (PASSES + g) : P, cols],
+                                start=(g == 0),
+                                stop=(g == PASSES - 1),
+                            )
+                        nc.vector.tensor_tensor(
+                            out=stage[:, :, s, cols],
+                            in0=acc[:].unsqueeze(1).to_broadcast([P, NR, N_TILE]),
+                            in1=review_sum[:, :, cols],
+                            op=ALU.add,
+                        )
+                for nr in range(NR):
+                    half = stage[:, nr].rearrange("p s o -> p (s o)")
+                    if group > 0 and nr == 1:
+                        nc.gpsimd.tensor_scalar(
+                            out=half, in0=half, scalar1=float("inf"), scalar2=0.0, op0=ALU.min, op1=ALU.max
+                        )
+                    else:
+                        nc.scalar.activation(out=half, in_=half, func=ACT.Relu)
+                    nc.sync.dma_start(
+                        out=out_rows[group, nr][:, :, first_mr * OUT : (first_mr + STEP_MR) * OUT], in_=half
+                    )
+
+        y_review = [None] * GROUPS
+        y_reply = [None] * GROUPS
+        for group in range(GROUPS):
+            engine = nc.vector if group == 0 else nc.gpsimd
+            y_review[group] = rotate(engine, x_review[group], "y_review%d" % group)
+            y_reply[group] = rotate(engine, x_reply[group], "y_reply%d" % group)
+        operands = pack(0, y_review[0], y_reply[0])
+        for group in range(GROUPS):
+            following = pack(group + 1, y_review[group + 1], y_reply[group + 1]) if group + 1 < GROUPS else None
+            table(group, *operands)
+            operands = following

@@ -27,9 +27,10 @@ J = P // POSITIONS
 GROUPS = BATCH // J
 NQ, NR = 8, 2
 MQ, MR = 2, 8
-STEP_MR = 2
 ROPE_BASE = 10000.0
 WRAPPED = 128
+LEAD = 4
+MAX_STEP = 2
 
 FLOPS = 2 * 2 * BATCH * POSITIONS * FEATURES * OUT
 
@@ -40,11 +41,14 @@ def tile_positionwisedtableencoder_kernel(tc, review, reply, W_words, W_scales, 
         const = ctx.enter_context(tc.tile_pool(name="const", bufs=1))
         inputs = ctx.enter_context(tc.tile_pool(name="inputs", bufs=1))
         rotated = ctx.enter_context(tc.tile_pool(name="rotated", bufs=1))
-        work = ctx.enter_context(tc.tile_pool(name="work", bufs=2))
+        work_v = ctx.enter_context(tc.tile_pool(name="work_v", bufs=1))
+        work_g = ctx.enter_context(tc.tile_pool(name="work_g", bufs=1))
+        grouped_pool = ctx.enter_context(tc.tile_pool(name="grouped", bufs=2))
         packed = ctx.enter_context(tc.tile_pool(name="packed", bufs=2))
-        stages = ctx.enter_context(tc.tile_pool(name="stages", bufs=4))
+        stages = ctx.enter_context(tc.tile_pool(name="stages", bufs=5))
         psum_t = ctx.enter_context(tc.psum_pool(name="psum_t", bufs=2))
         psum_acc = ctx.enter_context(tc.psum_pool(name="psum_acc", bufs=6))
+        ctx.enter_context(tc.manual_schedule())
 
         review_rows = review.rearrange("(g j) n h -> g (j n) h", j=J)
         reply_rows = reply.rearrange("(g j) m h -> g (j m) h", j=J)
@@ -52,6 +56,12 @@ def tile_positionwisedtableencoder_kernel(tc, review, reply, W_words, W_scales, 
         x_reply = [inputs.tile([P, FEATURES], BF16, name="x_reply%d" % g) for g in range(GROUPS)]
         nc.sync.dma_start(out=x_review[0][:], in_=review_rows[0])
         nc.sync.dma_start(out=x_reply[0][:], in_=reply_rows[0])
+
+        row_index = const.tile([P, 1], I32)
+        nc.gpsimd.iota(row_index[:], pattern=[[0, 1]], base=0, channel_multiplier=1)
+        warm = const.tile([P, 2], F32)
+        nc.vector.memset(warm[:, 0:1], 0.0)
+        nc.scalar.activation(out=warm[:, 1:2], in_=warm[:, 0:1], func=ACT.Sin)
 
         w_planes = const.tile([P, OUT], U8, align_bytes=64)
         nc.vector.memset(w_planes[:].bitcast(I32), 0)
@@ -69,8 +79,11 @@ def tile_positionwisedtableencoder_kernel(tc, review, reply, W_words, W_scales, 
             nc.sync.dma_start(out=x_review[g][:], in_=review_rows[g])
             nc.sync.dma_start(out=x_reply[g][:], in_=reply_rows[g])
 
-        row_index = const.tile([P, 1], I32)
-        nc.gpsimd.iota(row_index[:], pattern=[[0, 1]], base=0, channel_multiplier=1)
+        bias_rows = const.tile([P, OUT], BF16)
+        nc.gpsimd.memset(bias_rows[:], 0.0)
+        nc.scalar.dma_start(out=bias_rows[0:1, :], in_=b.rearrange("(one o) -> one o", one=1))
+        ones = const.tile([P, P], BF16)
+        nc.gpsimd.memset(ones[:], 1.0)
         identity = const.tile([P, P], F32)
         make_identity(nc, identity[:])
         order_review = const.tile([P, P], F32)
@@ -83,46 +96,36 @@ def tile_positionwisedtableencoder_kernel(tc, review, reply, W_words, W_scales, 
             out=order_reply[:].rearrange("p (r j q) -> p r j q", r=MR, j=J),
             in_=identity[:].rearrange("p (j q r) -> p r j q", j=J, r=MR),
         )
-        bias_rows = const.tile([P, OUT], BF16)
-        nc.gpsimd.memset(bias_rows[:], 0.0)
-        nc.scalar.dma_start(out=bias_rows[0:1, :], in_=b.rearrange("(one o) -> one o", one=1))
-        ones = const.tile([P, P], BF16)
-        nc.gpsimd.memset(ones[:], 1.0)
 
         position_int = const.tile([P, 1], I32)
         nc.vector.tensor_single_scalar(position_int[:], row_index[:], POSITIONS - 1, op=ALU.bitwise_and)
-        position = const.tile([P, 1], F32)
-        nc.vector.tensor_copy(out=position[:], in_=position_int[:])
-        frequency = const.tile([P, PAIRS], F32)
-        nc.vector.memset(frequency[:, 0:1], 1.0)
+        angle = const.tile([P, 2, PAIRS], F32)
+        nc.vector.tensor_copy(out=angle[:, 0, 0:1], in_=position_int[:])
         filled = 1
         while filled < PAIRS:
             nc.vector.tensor_scalar_mul(
-                out=frequency[:, filled : 2 * filled],
-                in0=frequency[:, 0:filled],
+                out=angle[:, 0, filled : 2 * filled],
+                in0=angle[:, 0, 0:filled],
                 scalar1=ROPE_BASE ** (-filled / PAIRS),
             )
             filled *= 2
-        angle = const.tile([P, 2, PAIRS], F32)
-        nc.vector.tensor_scalar_mul(out=angle[:, 0, :], in0=frequency[:], scalar1=position[:, 0:1])
-        nc.vector.tensor_scalar(
-            out=angle[:, 1, :], in0=frequency[:], scalar1=position[:, 0:1], scalar2=math.pi / 2,
-            op0=ALU.mult, op1=ALU.add,
-        )
+        nc.vector.tensor_scalar_add(out=angle[:, 1, :], in0=angle[:, 0, :], scalar1=math.pi / 2)
         turns = const.tile([P, 2, WRAPPED], I32)
         nc.vector.tensor_scalar_mul(out=turns[:], in0=angle[:, :, 0:WRAPPED], scalar1=1.0 / (2.0 * math.pi))
         nc.vector.scalar_tensor_tensor(
             out=angle[:, :, 0:WRAPPED], in0=turns[:], scalar=-2.0 * math.pi, in1=angle[:, :, 0:WRAPPED],
             op0=ALU.mult, op1=ALU.add,
         )
-        trig = const.tile([P, 2, PAIRS], F32)
-        nc.scalar.activation(
-            out=trig[:].rearrange("p t i -> p (t i)"), in_=angle[:].rearrange("p t i -> p (t i)"), func=ACT.Sin
-        )
-        sin = trig[:, 0, :]
-        cos = trig[:, 1, :]
-        minus_sin = const.tile([P, PAIRS], F32)
-        nc.vector.tensor_scalar_mul(out=minus_sin[:], in0=sin, scalar1=-1.0)
+        trig = const.tile([P, 3, PAIRS], F32)
+        cos = trig[:, 0, :]
+        minus_sin = trig[:, 1, :]
+        sin = trig[:, 2, :]
+        nc.scalar.activation(out=cos, in_=angle[:, 1, :], func=ACT.Sin)
+        nc.scalar.activation(out=minus_sin, in_=angle[:, 0, :], func=ACT.Sin, scale=-1.0)
+        nc.scalar.activation(out=sin, in_=angle[:, 0, :], func=ACT.Sin)
+
+        reply_planes = const.tile([P, PASSES * MR * J * 2 * MQ], U8, align_bytes=64)
+        nc.vector.memset(reply_planes[:].bitcast(I32), 0)
 
         bias_all = const.tile([P, OUT], F32)
         for h in range(HALVES):
@@ -131,17 +134,14 @@ def tile_positionwisedtableencoder_kernel(tc, review, reply, W_words, W_scales, 
             nc.tensor.matmul(spread[:], lhsT=ones[:], rhs=bias_rows[:, cols], start=True, stop=True)
             nc.scalar.copy(out=bias_all[:, cols], in_=spread[:])
 
-        reply_planes = const.tile([P, PASSES * MR * J * 2 * MQ], U8, align_bytes=64)
-        nc.vector.memset(reply_planes[:].bitcast(I32), 0)
-
-        def rotate(engine, x, name):
+        def rotate(engine, pool, x, name):
             pairs = x[:].rearrange("p (i e) -> p i e", e=2)
-            straight = work.tile([P, PAIRS, 2], F32, tag="straight")
-            crossed = work.tile([P, 2, PAIRS], F32, tag="crossed")
+            straight = pool.tile([P, PAIRS, 2], F32, tag="straight")
+            crossed = pool.tile([P, 2, PAIRS], F32, tag="crossed")
             engine.tensor_tensor(
                 out=straight[:], in0=pairs, in1=cos.unsqueeze(2).to_broadcast([P, PAIRS, 2]), op=ALU.mult
             )
-            engine.tensor_tensor(out=crossed[:, 0, :], in0=pairs[:, :, 1], in1=minus_sin[:], op=ALU.mult)
+            engine.tensor_tensor(out=crossed[:, 0, :], in0=pairs[:, :, 1], in1=minus_sin, op=ALU.mult)
             engine.tensor_tensor(out=crossed[:, 1, :], in0=pairs[:, :, 0], in1=sin, op=ALU.mult)
             y = rotated.tile([P, PAIRS, 2], BF16, name=name)
             engine.tensor_tensor(
@@ -159,9 +159,8 @@ def tile_positionwisedtableencoder_kernel(tc, review, reply, W_words, W_scales, 
                     )
             return planes
 
-        def pack(group, y_review, y_reply):
-            planes = transpose_words(y_review, order_review)
-            grouped = work.tile([P, PASSES, P, MQ, PACK], BF16, tag="grouped_review", align_bytes=64)
+        def copy_review(planes):
+            grouped = grouped_pool.tile([P, PASSES, P, MQ, PACK], BF16, tag="grouped_review", align_bytes=64)
             for g in range(PASSES):
                 nc.scalar.copy(
                     out=grouped[:, g].bitcast(F32),
@@ -170,6 +169,18 @@ def tile_positionwisedtableencoder_kernel(tc, review, reply, W_words, W_scales, 
                     .unsqueeze(2)
                     .to_broadcast([P, P, MQ, 2]),
                 )
+            return grouped
+
+        def copy_reply(planes):
+            grouped = grouped_pool.tile([P, PASSES, MR * J, 2, MQ, PACK], BF16, tag="grouped_reply", align_bytes=64)
+            for twin in range(2):
+                nc.scalar.copy(
+                    out=grouped[:, :, :, twin, :, :].bitcast(F32),
+                    in_=planes[:].rearrange("p (g u) (a q) -> p g a q u", u=2, q=MQ),
+                )
+            return grouped
+
+        def quantize_review(grouped):
             review_codes = packed.tile([P, PASSES * NR * P], I32, tag="review_codes", align_bytes=64)
             review_planes = packed.tile([P, PASSES * NR * P], U8, tag="review_planes", align_bytes=64)
             nc.vector.quantize_mx(
@@ -177,20 +188,18 @@ def tile_positionwisedtableencoder_kernel(tc, review, reply, W_words, W_scales, 
                 scales=review_planes[:],
                 in_=grouped[:].rearrange("p g c r t -> p (g c r t)"),
             )
+            return review_codes, review_planes
 
-            planes = transpose_words(y_reply, order_reply)
-            grouped = work.tile([P, PASSES, MR * J, 2, MQ, PACK], BF16, tag="grouped_reply", align_bytes=64)
-            for twin in range(2):
-                nc.scalar.copy(
-                    out=grouped[:, :, :, twin, :, :].bitcast(F32),
-                    in_=planes[:].rearrange("p (g u) (a q) -> p g a q u", u=2, q=MQ),
-                )
+        def quantize_reply(grouped):
             reply_codes = packed.tile([P, PASSES * MR * J * 2 * MQ], I32, tag="reply_codes", align_bytes=64)
             nc.vector.quantize_mx(
                 out=reply_codes[:].bitcast(FP8X4),
                 scales=reply_planes[:],
                 in_=grouped[:].rearrange("p g a r q t -> p (g a r q t)"),
             )
+            return reply_codes
+
+        def spread_reply(reply_codes):
             spread_codes = packed.tile([P, PASSES, MR, P], I32, tag="spread_codes", align_bytes=64)
             spread_planes = packed.tile([P, PASSES, MR, P], U8, tag="spread_planes", align_bytes=64)
             nc.vector.tensor_copy(
@@ -204,76 +213,145 @@ def tile_positionwisedtableencoder_kernel(tc, review, reply, W_words, W_scales, 
                 out=spread_planes[:].bitcast(I32).rearrange("p g r (j a) -> p (g r j) a", a=NQ // 2),
                 in_=reply_planes[:].bitcast(I32).unsqueeze(2).to_broadcast([P, PASSES * MR * J, NQ // 2]),
             )
+            return spread_codes, spread_planes
 
-            review_sum = packed.tile([P, NR, OUT], F32, tag="review_sum")
-            for nr in range(NR):
-                for h in range(HALVES):
-                    cols = slice(h * N_TILE, (h + 1) * N_TILE)
-                    acc = psum_acc.tile([P, N_TILE], F32, tag="acc")
-                    for g in range(PASSES):
-                        block = slice((g * NR + nr) * P, (g * NR + nr + 1) * P)
-                        nc.tensor.matmul_mx(
-                            out=acc[:],
-                            lhsT=review_codes[:, block].bitcast(FP8X4),
-                            lhsT_scale=review_planes[:, block],
-                            rhs=w_codes[:, g, cols].bitcast(FP8X4),
-                            rhs_scale=w_planes[4 * g : P, cols],
-                            start=(g == 0),
-                            stop=(g == PASSES - 1),
-                        )
-                    nc.vector.tensor_tensor(
-                        out=review_sum[:, nr, cols], in0=acc[:], in1=bias_all[:, cols], op=ALU.add
-                    )
-            return spread_codes, spread_planes, review_sum
+        def multiply(codes, planes, first_pass, h):
+            cols = slice(h * N_TILE, (h + 1) * N_TILE)
+            acc = psum_acc.tile([P, N_TILE], F32, tag="acc")
+            for g in range(PASSES):
+                nc.tensor.matmul_mx(
+                    out=acc[:],
+                    lhsT=codes[g].bitcast(FP8X4),
+                    lhsT_scale=planes[g],
+                    rhs=w_codes[:, first_pass + g, cols].bitcast(FP8X4),
+                    rhs_scale=w_planes[4 * (first_pass + g) : P, cols],
+                    start=(g == 0),
+                    stop=(g == PASSES - 1),
+                )
+            return acc
+
+        def multiply_review(operands, bank):
+            nr, h = bank // HALVES, bank % HALVES
+            review_codes, review_planes = operands
+            blocks = [slice((g * NR + nr) * P, (g * NR + nr + 1) * P) for g in range(PASSES)]
+            return multiply(
+                [review_codes[:, block] for block in blocks], [review_planes[:, block] for block in blocks], 0, h
+            )
+
+        def multiply_reply(operands, bank):
+            mr, h = bank // HALVES, bank % HALVES
+            spread_codes, spread_planes = operands
+            return multiply(
+                [spread_codes[:, g, mr, :] for g in range(PASSES)],
+                [spread_planes[:, g, mr, :] for g in range(PASSES)],
+                PASSES,
+                h,
+            )
+
+        def add_bias(review_sum, bank, acc):
+            nr, h = bank // HALVES, bank % HALVES
+            cols = slice(h * N_TILE, (h + 1) * N_TILE)
+            nc.vector.tensor_tensor(out=review_sum[:, nr, cols], in0=acc[:], in1=bias_all[:, cols], op=ALU.add)
+
+        gate = const.tile([P, 1], I32)
+
+        def hold_gpsimd(spread_planes):
+            nc.gpsimd.tensor_copy(out=gate[:], in_=spread_planes[:, 0, 0, 0:4].bitcast(I32))
 
         out_rows = out.rearrange(
             "(g j) (nq nr) (mq mr) o -> g nr (j nq) mq (mr o)", j=J, nr=NR, mq=MQ
         )
-
-        def table(group, spread_codes, spread_planes, review_sum):
-            for first_mr in range(0, MR, STEP_MR):
-                stage = stages.tile([P, NR, STEP_MR, OUT], F32, tag="stage")
-                for s in range(STEP_MR):
-                    mr = first_mr + s
-                    for h in range(HALVES):
-                        cols = slice(h * N_TILE, (h + 1) * N_TILE)
-                        acc = psum_acc.tile([P, N_TILE], F32, tag="acc")
-                        for g in range(PASSES):
-                            nc.tensor.matmul_mx(
-                                out=acc[:],
-                                lhsT=spread_codes[:, g, mr, :].bitcast(FP8X4),
-                                lhsT_scale=spread_planes[:, g, mr, :],
-                                rhs=w_codes[:, PASSES + g, cols].bitcast(FP8X4),
-                                rhs_scale=w_planes[4 * (PASSES + g) : P, cols],
-                                start=(g == 0),
-                                stop=(g == PASSES - 1),
-                            )
-                        nc.vector.tensor_tensor(
-                            out=stage[:, :, s, cols],
-                            in0=acc[:].unsqueeze(1).to_broadcast([P, NR, N_TILE]),
-                            in1=review_sum[:, :, cols],
-                            op=ALU.add,
-                        )
-                for nr in range(NR):
-                    half = stage[:, nr].rearrange("p s o -> p (s o)")
-                    if group > 0 and nr == 1:
-                        nc.gpsimd.tensor_scalar(
-                            out=half, in0=half, scalar1=float("inf"), scalar2=0.0, op0=ALU.min, op1=ALU.max
-                        )
-                    else:
-                        nc.scalar.activation(out=half, in_=half, func=ACT.Relu)
-                    nc.sync.dma_start(
-                        out=out_rows[group, nr][:, :, first_mr * OUT : (first_mr + STEP_MR) * OUT], in_=half
-                    )
-
+        BANKS = MR * HALVES
+        REVIEW_BANKS = NR * HALVES
         y_review = [None] * GROUPS
         y_reply = [None] * GROUPS
+        grouped_review = [None] * GROUPS
+        grouped_reply = [None] * GROUPS
+        review_operands = [None] * GROUPS
+        reply_operands = [None] * GROUPS
+        review_sums = [None] * GROUPS
+        review_accs = {}
+        reply_accs = {}
+
+        def finish_preparation(group):
+            reply_codes = quantize_reply(grouped_reply[group])
+            review_sum = packed.tile([P, NR, OUT], F32, tag="review_sum")
+            review_sums[group] = review_sum
+            add_bias(review_sum, 0, review_accs[(group, 0)])
+            add_bias(review_sum, 1, review_accs[(group, 1)])
+            reply_operands[group] = spread_reply(reply_codes)
+            if group + 1 < GROUPS:
+                hold_gpsimd(reply_operands[group][1])
+                y_review[group + 1] = rotate(nc.gpsimd, work_g, x_review[group + 1], "y_review%d" % (group + 1))
+                y_reply[group + 1] = rotate(nc.gpsimd, work_g, x_reply[group + 1], "y_reply%d" % (group + 1))
+            reply_accs[(group, 0)] = multiply_reply(reply_operands[group], 0)
+            reply_accs[(group, 1)] = multiply_reply(reply_operands[group], 1)
+            add_bias(review_sum, 2, review_accs[(group, 2)])
+            reply_accs[(group, 2)] = multiply_reply(reply_operands[group], 2)
+            add_bias(review_sum, 3, review_accs[(group, 3)])
+            reply_accs[(group, 3)] = multiply_reply(reply_operands[group], 3)
+
+        def table(group, steps):
+            following = group + 1
+            step_at = {}
+            first = 0
+            for step in steps:
+                step_at[first] = step
+                first += step
+            stage = None
+            first_mr = 0
+            for bank in range(BANKS):
+                mr, h = bank // HALVES, bank % HALVES
+                cols = slice(h * N_TILE, (h + 1) * N_TILE)
+                if bank + LEAD < BANKS:
+                    reply_accs[(group, bank + LEAD)] = multiply_reply(reply_operands[group], bank + LEAD)
+                elif following < GROUPS:
+                    review_accs[(following, bank + LEAD - BANKS)] = multiply_review(
+                        review_operands[following], bank + LEAD - BANKS
+                    )
+                if following < GROUPS and bank == 7:
+                    planes_review = transpose_words(y_review[following], order_review)
+                if following < GROUPS and bank == 11:
+                    planes_reply = transpose_words(y_reply[following], order_reply)
+                if h == 0 and mr in step_at:
+                    stage = stages.tile([P, NR, MAX_STEP, OUT], F32, tag="stage")
+                    first_mr = mr
+                s = mr - first_mr
+                nc.vector.tensor_tensor(
+                    out=stage[:, :, s, cols],
+                    in0=reply_accs[(group, bank)][:].unsqueeze(1).to_broadcast([P, NR, N_TILE]),
+                    in1=review_sums[group][:, :, cols],
+                    op=ALU.add,
+                )
+                if h == HALVES - 1:
+                    last = group == GROUPS - 1 and mr == MR - 1
+                    if last:
+                        nc.scalar.activation(out=stage[:, 0, s, :], in_=stage[:, 0, s, :], func=ACT.Relu)
+                        nc.gpsimd.tensor_scalar(
+                            out=stage[:, 1, s, :], in0=stage[:, 1, s, :],
+                            scalar1=float("inf"), scalar2=0.0, op0=ALU.min, op1=ALU.max,
+                        )
+                    else:
+                        nc.scalar.activation(out=stage[:, :, s, :], in_=stage[:, :, s, :], func=ACT.Relu)
+                    if s == step_at[first_mr] - 1:
+                        for nr in range(NR):
+                            nc.sync.dma_start(
+                                out=out_rows[group, nr][:, :, first_mr * OUT : (mr + 1) * OUT],
+                                in_=stage[:, nr, 0 : s + 1, :].rearrange("p s o -> p (s o)"),
+                            )
+                if following < GROUPS and bank == 7:
+                    grouped_review[following] = copy_review(planes_review)
+                if following < GROUPS and bank == 11:
+                    grouped_reply[following] = copy_reply(planes_reply)
+                    review_operands[following] = quantize_review(grouped_review[following])
+
+        y_review[0] = rotate(nc.vector, work_v, x_review[0], "y_review0")
+        grouped_review[0] = copy_review(transpose_words(y_review[0], order_review))
+        y_reply[0] = rotate(nc.vector, work_v, x_reply[0], "y_reply0")
+        grouped_reply[0] = copy_reply(transpose_words(y_reply[0], order_reply))
+        review_operands[0] = quantize_review(grouped_review[0])
+        for bank in range(REVIEW_BANKS):
+            review_accs[(0, bank)] = multiply_review(review_operands[0], bank)
         for group in range(GROUPS):
-            engine = nc.vector if group == 0 else nc.gpsimd
-            y_review[group] = rotate(engine, x_review[group], "y_review%d" % group)
-            y_reply[group] = rotate(engine, x_reply[group], "y_reply%d" % group)
-        operands = pack(0, y_review[0], y_reply[0])
-        for group in range(GROUPS):
-            following = pack(group + 1, y_review[group + 1], y_reply[group + 1]) if group + 1 < GROUPS else None
-            table(group, *operands)
-            operands = following
+            finish_preparation(group)
+            table(group, [2, 2, 2, 1, 1] if group == GROUPS - 1 else [2, 2, 2, 2])

@@ -2,7 +2,6 @@ from contextlib import ExitStack
 import math
 
 import concourse.mybir as mybir
-from concourse.masks import make_identity
 
 F32 = mybir.dt.float32
 BF16 = mybir.dt.bfloat16
@@ -29,8 +28,10 @@ NQ, NR = 8, 2
 MQ, MR = 2, 8
 ROPE_BASE = 10000.0
 WRAPPED = 128
+LOW = 32
+HIGH = PAIRS // LOW
 LEAD = 4
-MAX_STEP = 2
+MAX_STEP = 1
 
 FLOPS = 2 * 2 * BATCH * POSITIONS * FEATURES * OUT
 
@@ -45,7 +46,7 @@ def tile_positionwisedtableencoder_kernel(tc, review, reply, W_words, W_scales, 
         work_g = ctx.enter_context(tc.tile_pool(name="work_g", bufs=1))
         grouped_pool = ctx.enter_context(tc.tile_pool(name="grouped", bufs=2))
         packed = ctx.enter_context(tc.tile_pool(name="packed", bufs=2))
-        stages = ctx.enter_context(tc.tile_pool(name="stages", bufs=5))
+        stages = ctx.enter_context(tc.tile_pool(name="stages", bufs=10))
         psum_t = ctx.enter_context(tc.psum_pool(name="psum_t", bufs=2))
         psum_acc = ctx.enter_context(tc.psum_pool(name="psum_acc", bufs=6))
         ctx.enter_context(tc.manual_schedule())
@@ -56,6 +57,9 @@ def tile_positionwisedtableencoder_kernel(tc, review, reply, W_words, W_scales, 
         x_reply = [inputs.tile([P, FEATURES], BF16, name="x_reply%d" % g) for g in range(GROUPS)]
         nc.sync.dma_start(out=x_review[0][:], in_=review_rows[0])
         nc.sync.dma_start(out=x_reply[0][:], in_=reply_rows[0])
+        bias_rows = const.tile([P, OUT], BF16)
+        nc.vector.memset(bias_rows[:], 0.0)
+        nc.sync.dma_start(out=bias_rows[0:1, :], in_=b.rearrange("(one o) -> one o", one=1))
 
         row_index = const.tile([P, 1], I32)
         nc.gpsimd.iota(row_index[:], pattern=[[0, 1]], base=0, channel_multiplier=1)
@@ -79,50 +83,73 @@ def tile_positionwisedtableencoder_kernel(tc, review, reply, W_words, W_scales, 
             nc.sync.dma_start(out=x_review[g][:], in_=review_rows[g])
             nc.sync.dma_start(out=x_reply[g][:], in_=reply_rows[g])
 
-        bias_rows = const.tile([P, OUT], BF16)
-        nc.gpsimd.memset(bias_rows[:], 0.0)
-        nc.scalar.dma_start(out=bias_rows[0:1, :], in_=b.rearrange("(one o) -> one o", one=1))
         ones = const.tile([P, P], BF16)
         nc.gpsimd.memset(ones[:], 1.0)
-        identity = const.tile([P, P], F32)
-        make_identity(nc, identity[:])
-        order_review = const.tile([P, P], F32)
-        nc.gpsimd.tensor_copy(
-            out=order_review[:].rearrange("p (r j q) -> p r j q", r=NR, j=J),
-            in_=identity[:].rearrange("p (j q r) -> p r j q", j=J, r=NR),
+        offsets = const.tile([P, 2, P], I32)
+        nc.gpsimd.iota(
+            offsets[:, 0, :], pattern=[[1, NR], [POSITIONS, J], [NR, NQ]], base=0, channel_multiplier=-1
         )
-        order_reply = const.tile([P, P], F32)
-        nc.gpsimd.tensor_copy(
-            out=order_reply[:].rearrange("p (r j q) -> p r j q", r=MR, j=J),
-            in_=identity[:].rearrange("p (j q r) -> p r j q", j=J, r=MR),
+        nc.gpsimd.iota(
+            offsets[:, 1, :], pattern=[[1, MR], [POSITIONS, J], [MR, MQ]], base=0, channel_multiplier=-1
         )
 
+        low = const.tile([P, LOW], F32)
+        high = const.tile([P, HIGH], F32)
+        nc.vector.memset(low[:, 0:1], 1.0)
+        nc.vector.memset(high[:, 0:1], 1.0)
+        filled = 1
+        while filled < LOW:
+            nc.vector.tensor_scalar_mul(
+                out=low[:, filled : 2 * filled], in0=low[:, 0:filled], scalar1=ROPE_BASE ** (-filled / PAIRS)
+            )
+            if filled < HIGH:
+                nc.vector.tensor_scalar_mul(
+                    out=high[:, filled : 2 * filled],
+                    in0=high[:, 0:filled],
+                    scalar1=ROPE_BASE ** (-filled * LOW / PAIRS),
+                )
+            filled *= 2
         position_int = const.tile([P, 1], I32)
         nc.vector.tensor_single_scalar(position_int[:], row_index[:], POSITIONS - 1, op=ALU.bitwise_and)
-        angle = const.tile([P, 2, PAIRS], F32)
-        nc.vector.tensor_copy(out=angle[:, 0, 0:1], in_=position_int[:])
-        filled = 1
-        while filled < PAIRS:
-            nc.vector.tensor_scalar_mul(
-                out=angle[:, 0, filled : 2 * filled],
-                in0=angle[:, 0, 0:filled],
-                scalar1=ROPE_BASE ** (-filled / PAIRS),
-            )
-            filled *= 2
-        nc.vector.tensor_scalar_add(out=angle[:, 1, :], in0=angle[:, 0, :], scalar1=math.pi / 2)
-        turns = const.tile([P, 2, WRAPPED], I32)
-        nc.vector.tensor_scalar_mul(out=turns[:], in0=angle[:, :, 0:WRAPPED], scalar1=1.0 / (2.0 * math.pi))
+        position = const.tile([P, 1], F32)
+        nc.vector.tensor_copy(out=position[:], in_=position_int[:])
+        angle = const.tile([P, PAIRS], F32)
         nc.vector.scalar_tensor_tensor(
-            out=angle[:, :, 0:WRAPPED], in0=turns[:], scalar=-2.0 * math.pi, in1=angle[:, :, 0:WRAPPED],
+            out=angle[:].rearrange("p (a b) -> p a b", b=LOW),
+            in0=high[:].unsqueeze(2).to_broadcast([P, HIGH, LOW]),
+            scalar=position[:, 0:1],
+            in1=low[:].unsqueeze(1).to_broadcast([P, HIGH, LOW]),
+            op0=ALU.mult,
+            op1=ALU.mult,
+        )
+        turns = const.tile([P, 2, WRAPPED], I32)
+        nc.vector.tensor_scalar_mul(out=turns[:, 0, :], in0=angle[:, 0:WRAPPED], scalar1=1.0 / (2.0 * math.pi))
+        nc.vector.tensor_scalar(
+            out=turns[:, 1, :], in0=angle[:, 0:WRAPPED], scalar1=1.0 / (2.0 * math.pi), scalar2=0.25,
             op0=ALU.mult, op1=ALU.add,
         )
+        wrapped = const.tile([P, 2, WRAPPED], F32)
+        for plane in range(2):
+            nc.vector.scalar_tensor_tensor(
+                out=wrapped[:, plane, :], in0=turns[:, plane, :], scalar=-2.0 * math.pi, in1=angle[:, 0:WRAPPED],
+                op0=ALU.mult, op1=ALU.add,
+            )
         trig = const.tile([P, 3, PAIRS], F32)
         cos = trig[:, 0, :]
         minus_sin = trig[:, 1, :]
         sin = trig[:, 2, :]
-        nc.scalar.activation(out=cos, in_=angle[:, 1, :], func=ACT.Sin)
-        nc.scalar.activation(out=minus_sin, in_=angle[:, 0, :], func=ACT.Sin, scale=-1.0)
-        nc.scalar.activation(out=sin, in_=angle[:, 0, :], func=ACT.Sin)
+        rest = slice(WRAPPED, PAIRS)
+        nc.scalar.activation(out=trig[:, 0, rest], in_=angle[:, rest], func=ACT.Sin, bias=math.pi / 2)
+        nc.scalar.activation(out=trig[:, 1, rest], in_=angle[:, rest], func=ACT.Sin, scale=-1.0)
+        nc.scalar.activation(out=trig[:, 0, 0:WRAPPED], in_=wrapped[:, 1, :], func=ACT.Sin, bias=math.pi / 2)
+        nc.scalar.activation(out=trig[:, 1, 0:WRAPPED], in_=wrapped[:, 0, :], func=ACT.Sin, scale=-1.0)
+        nc.scalar.activation(out=trig[:, 2, rest], in_=angle[:, rest], func=ACT.Sin)
+        nc.scalar.activation(out=trig[:, 2, 0:WRAPPED], in_=wrapped[:, 0, :], func=ACT.Sin)
+
+        orders = const.tile([P, 2, P], F32)
+        nc.vector.tensor_single_scalar(orders[:], offsets[:], 0, op=ALU.is_equal)
+        order_review = orders[:, 0, :]
+        order_reply = orders[:, 1, :]
 
         reply_planes = const.tile([P, PASSES * MR * J * 2 * MQ], U8, align_bytes=64)
         nc.vector.memset(reply_planes[:].bitcast(I32), 0)
@@ -134,7 +161,7 @@ def tile_positionwisedtableencoder_kernel(tc, review, reply, W_words, W_scales, 
             nc.tensor.matmul(spread[:], lhsT=ones[:], rhs=bias_rows[:, cols], start=True, stop=True)
             nc.scalar.copy(out=bias_all[:, cols], in_=spread[:])
 
-        def rotate(engine, pool, x, name):
+        def rotary_products(engine, pool, x):
             pairs = x[:].rearrange("p (i e) -> p i e", e=2)
             straight = pool.tile([P, PAIRS, 2], F32, tag="straight")
             crossed = pool.tile([P, 2, PAIRS], F32, tag="crossed")
@@ -143,11 +170,18 @@ def tile_positionwisedtableencoder_kernel(tc, review, reply, W_words, W_scales, 
             )
             engine.tensor_tensor(out=crossed[:, 0, :], in0=pairs[:, :, 1], in1=minus_sin, op=ALU.mult)
             engine.tensor_tensor(out=crossed[:, 1, :], in0=pairs[:, :, 0], in1=sin, op=ALU.mult)
+            return straight, crossed
+
+        def rotary_sum(engine, products, name):
+            straight, crossed = products
             y = rotated.tile([P, PAIRS, 2], BF16, name=name)
             engine.tensor_tensor(
                 out=y[:], in0=straight[:], in1=crossed[:].rearrange("p e i -> p i e"), op=ALU.add
             )
             return y
+
+        def rotate(engine, pool, x, name):
+            return rotary_sum(engine, rotary_products(engine, pool, x), name)
 
         def transpose_words(y, order):
             words = y[:].rearrange("p i e -> p (i e)").bitcast(F32)
@@ -155,7 +189,7 @@ def tile_positionwisedtableencoder_kernel(tc, review, reply, W_words, W_scales, 
             for g in range(PASSES):
                 for u in range(2):
                     nc.tensor.transpose(
-                        planes[:, 2 * g + u, :], words[:, 256 * g + u : 256 * (g + 1) : 2], order[:]
+                        planes[:, 2 * g + u, :], words[:, 256 * g + u : 256 * (g + 1) : 2], order
                     )
             return planes
 
@@ -274,11 +308,15 @@ def tile_positionwisedtableencoder_kernel(tc, review, reply, W_words, W_scales, 
         reply_accs = {}
 
         def finish_preparation(group):
-            reply_codes = quantize_reply(grouped_reply[group])
             review_sum = packed.tile([P, NR, OUT], F32, tag="review_sum")
             review_sums[group] = review_sum
-            add_bias(review_sum, 0, review_accs[(group, 0)])
-            add_bias(review_sum, 1, review_accs[(group, 1)])
+            early = 2 if group == 0 else 0
+            for bank in range(early):
+                add_bias(review_sum, bank, review_accs[(group, bank)])
+            reply_codes = quantize_reply(grouped_reply[group])
+            for bank in range(early, REVIEW_BANKS - 2 + early // 2):
+                add_bias(review_sum, bank, review_accs[(group, bank)])
+            late = REVIEW_BANKS - 2 + early // 2
             reply_operands[group] = spread_reply(reply_codes)
             if group + 1 < GROUPS:
                 hold_gpsimd(reply_operands[group][1])
@@ -286,9 +324,9 @@ def tile_positionwisedtableencoder_kernel(tc, review, reply, W_words, W_scales, 
                 y_reply[group + 1] = rotate(nc.gpsimd, work_g, x_reply[group + 1], "y_reply%d" % (group + 1))
             reply_accs[(group, 0)] = multiply_reply(reply_operands[group], 0)
             reply_accs[(group, 1)] = multiply_reply(reply_operands[group], 1)
-            add_bias(review_sum, 2, review_accs[(group, 2)])
+            for bank in range(late, REVIEW_BANKS):
+                add_bias(review_sum, bank, review_accs[(group, bank)])
             reply_accs[(group, 2)] = multiply_reply(reply_operands[group], 2)
-            add_bias(review_sum, 3, review_accs[(group, 3)])
             reply_accs[(group, 3)] = multiply_reply(reply_operands[group], 3)
 
         def table(group, steps):
@@ -323,9 +361,22 @@ def tile_positionwisedtableencoder_kernel(tc, review, reply, W_words, W_scales, 
                     in1=review_sums[group][:, :, cols],
                     op=ALU.add,
                 )
-                if h == HALVES - 1:
-                    last = group == GROUPS - 1 and mr == MR - 1
-                    if last:
+                if group == GROUPS - 1 and mr == MR - 1:
+                    if h < HALVES - 1:
+                        nc.scalar.activation(out=stage[:, :, s, cols], in_=stage[:, :, s, cols], func=ACT.Relu)
+                    else:
+                        nc.scalar.activation(out=stage[:, 0, s, cols], in_=stage[:, 0, s, cols], func=ACT.Relu)
+                        nc.gpsimd.tensor_scalar(
+                            out=stage[:, 1, s, cols], in0=stage[:, 1, s, cols],
+                            scalar1=float("inf"), scalar2=0.0, op0=ALU.min, op1=ALU.max,
+                        )
+                    for nr in range(NR):
+                        nc.sync.dma_start(
+                            out=out_rows[group, nr][:, :, mr * OUT + h * N_TILE : mr * OUT + (h + 1) * N_TILE],
+                            in_=stage[:, nr, s, cols],
+                        )
+                elif h == HALVES - 1:
+                    if following == GROUPS:
                         nc.scalar.activation(out=stage[:, 0, s, :], in_=stage[:, 0, s, :], func=ACT.Relu)
                         nc.gpsimd.tensor_scalar(
                             out=stage[:, 1, s, :], in0=stage[:, 1, s, :],
@@ -347,11 +398,14 @@ def tile_positionwisedtableencoder_kernel(tc, review, reply, W_words, W_scales, 
 
         y_review[0] = rotate(nc.vector, work_v, x_review[0], "y_review0")
         grouped_review[0] = copy_review(transpose_words(y_review[0], order_review))
-        y_reply[0] = rotate(nc.vector, work_v, x_reply[0], "y_reply0")
-        grouped_reply[0] = copy_reply(transpose_words(y_reply[0], order_reply))
+        products = rotary_products(nc.vector, work_v, x_reply[0])
         review_operands[0] = quantize_review(grouped_review[0])
-        for bank in range(REVIEW_BANKS):
+        for bank in range(REVIEW_BANKS // 2):
+            review_accs[(0, bank)] = multiply_review(review_operands[0], bank)
+        y_reply[0] = rotary_sum(nc.vector, products, "y_reply0")
+        grouped_reply[0] = copy_reply(transpose_words(y_reply[0], order_reply))
+        for bank in range(REVIEW_BANKS // 2, REVIEW_BANKS):
             review_accs[(0, bank)] = multiply_review(review_operands[0], bank)
         for group in range(GROUPS):
             finish_preparation(group)
-            table(group, [2, 2, 2, 1, 1] if group == GROUPS - 1 else [2, 2, 2, 2])
+            table(group, [1] * 8)

@@ -31,6 +31,9 @@ WRAPPED = 128
 LOW = 32
 HIGH = PAIRS // LOW
 LEAD = 4
+QUANTIZE_AT = 12
+PARTS = 2
+PART_MR = MR // PARTS
 MAX_STEP = 1
 
 FLOPS = 2 * 2 * BATCH * POSITIONS * FEATURES * OUT
@@ -55,33 +58,23 @@ def tile_positionwisedtableencoder_kernel(tc, review, reply, W_words, W_scales, 
         reply_rows = reply.rearrange("(g j) m h -> g (j m) h", j=J)
         x_review = [inputs.tile([P, FEATURES], BF16, name="x_review%d" % g) for g in range(GROUPS)]
         x_reply = [inputs.tile([P, FEATURES], BF16, name="x_reply%d" % g) for g in range(GROUPS)]
-        nc.sync.dma_start(out=x_review[0][:], in_=review_rows[0])
+        nc.scalar.dma_start(out=x_review[0][:], in_=review_rows[0])
         nc.sync.dma_start(out=x_reply[0][:], in_=reply_rows[0])
-        bias_rows = const.tile([P, OUT], BF16)
-        nc.vector.memset(bias_rows[:], 0.0)
-        nc.sync.dma_start(out=bias_rows[0:1, :], in_=b.rearrange("(one o) -> one o", one=1))
+        w_codes = const.tile([P, 2 * PASSES, OUT], I32, align_bytes=64)
+
+        def load_codes(g):
+            nc.sync.dma_start(
+                out=w_codes[:, g, :], in_=W_words[g].rearrange("p n t -> p (n t)").bitcast(I32)
+            )
+
+        for g in range(PASSES):
+            load_codes(g)
 
         row_index = const.tile([P, 1], I32)
         nc.gpsimd.iota(row_index[:], pattern=[[0, 1]], base=0, channel_multiplier=1)
         warm = const.tile([P, 2], F32)
         nc.vector.memset(warm[:, 0:1], 0.0)
         nc.scalar.activation(out=warm[:, 1:2], in_=warm[:, 0:1], func=ACT.Sin)
-
-        w_planes = const.tile([P, OUT], U8, align_bytes=64)
-        nc.vector.memset(w_planes[:].bitcast(I32), 0)
-        for quadrant in range(4):
-            nc.sync.dma_start(
-                out=w_planes[32 * quadrant : 32 * quadrant + 16, :].bitcast(I32),
-                in_=W_scales[:, 4 * quadrant : 4 * quadrant + 4, :].bitcast(I32),
-            )
-        w_codes = const.tile([P, 2 * PASSES, OUT], I32, align_bytes=64)
-        for g in range(2 * PASSES):
-            nc.sync.dma_start(
-                out=w_codes[:, g, :], in_=W_words[g].rearrange("p n t -> p (n t)").bitcast(I32)
-            )
-        for g in range(1, GROUPS):
-            nc.sync.dma_start(out=x_review[g][:], in_=review_rows[g])
-            nc.sync.dma_start(out=x_reply[g][:], in_=reply_rows[g])
 
         ones = const.tile([P, P], BF16)
         nc.gpsimd.memset(ones[:], 1.0)
@@ -123,11 +116,11 @@ def tile_positionwisedtableencoder_kernel(tc, review, reply, W_words, W_scales, 
             op1=ALU.mult,
         )
         turns = const.tile([P, 2, WRAPPED], I32)
-        nc.vector.tensor_scalar_mul(out=turns[:, 0, :], in0=angle[:, 0:WRAPPED], scalar1=1.0 / (2.0 * math.pi))
         nc.vector.tensor_scalar(
-            out=turns[:, 1, :], in0=angle[:, 0:WRAPPED], scalar1=1.0 / (2.0 * math.pi), scalar2=0.25,
+            out=turns[:, 0, :], in0=angle[:, 0:WRAPPED], scalar1=1.0 / (2.0 * math.pi), scalar2=0.25,
             op0=ALU.mult, op1=ALU.add,
         )
+        nc.vector.tensor_scalar_mul(out=turns[:, 1, :], in0=angle[:, 0:WRAPPED], scalar1=1.0 / (2.0 * math.pi))
         wrapped = const.tile([P, 2, WRAPPED], F32)
         for plane in range(2):
             nc.vector.scalar_tensor_tensor(
@@ -140,11 +133,27 @@ def tile_positionwisedtableencoder_kernel(tc, review, reply, W_words, W_scales, 
         sin = trig[:, 2, :]
         rest = slice(WRAPPED, PAIRS)
         nc.scalar.activation(out=trig[:, 0, rest], in_=angle[:, rest], func=ACT.Sin, bias=math.pi / 2)
+        nc.scalar.activation(out=trig[:, 0, 0:WRAPPED], in_=wrapped[:, 0, :], func=ACT.Sin, bias=math.pi / 2)
         nc.scalar.activation(out=trig[:, 1, rest], in_=angle[:, rest], func=ACT.Sin, scale=-1.0)
-        nc.scalar.activation(out=trig[:, 0, 0:WRAPPED], in_=wrapped[:, 1, :], func=ACT.Sin, bias=math.pi / 2)
-        nc.scalar.activation(out=trig[:, 1, 0:WRAPPED], in_=wrapped[:, 0, :], func=ACT.Sin, scale=-1.0)
+        nc.scalar.activation(out=trig[:, 1, 0:WRAPPED], in_=wrapped[:, 1, :], func=ACT.Sin, scale=-1.0)
         nc.scalar.activation(out=trig[:, 2, rest], in_=angle[:, rest], func=ACT.Sin)
-        nc.scalar.activation(out=trig[:, 2, 0:WRAPPED], in_=wrapped[:, 0, :], func=ACT.Sin)
+        nc.scalar.activation(out=trig[:, 2, 0:WRAPPED], in_=wrapped[:, 1, :], func=ACT.Sin)
+
+        bias_rows = const.tile([P, OUT], BF16)
+        nc.vector.memset(bias_rows[:], 0.0)
+        nc.sync.dma_start(out=bias_rows[0:1, :], in_=b.rearrange("(one o) -> one o", one=1))
+        w_planes = const.tile([P, OUT], U8, align_bytes=64)
+        nc.vector.memset(w_planes[:].bitcast(I32), 0)
+        for quadrant in range(4):
+            nc.sync.dma_start(
+                out=w_planes[32 * quadrant : 32 * quadrant + 16, :].bitcast(I32),
+                in_=W_scales[:, 4 * quadrant : 4 * quadrant + 4, :].bitcast(I32),
+            )
+        for g in range(PASSES, 2 * PASSES):
+            load_codes(g)
+        for g in range(1, GROUPS):
+            nc.sync.dma_start(out=x_review[g][:], in_=review_rows[g])
+            nc.sync.dma_start(out=x_reply[g][:], in_=reply_rows[g])
 
         orders = const.tile([P, 2, P], F32)
         nc.vector.tensor_single_scalar(orders[:], offsets[:], 0, op=ALU.is_equal)
@@ -206,12 +215,18 @@ def tile_positionwisedtableencoder_kernel(tc, review, reply, W_words, W_scales, 
             return grouped
 
         def copy_reply(planes):
-            grouped = grouped_pool.tile([P, PASSES, MR * J, 2, MQ, PACK], BF16, tag="grouped_reply", align_bytes=64)
-            for twin in range(2):
-                nc.scalar.copy(
-                    out=grouped[:, :, :, twin, :, :].bitcast(F32),
-                    in_=planes[:].rearrange("p (g u) (a q) -> p g a q u", u=2, q=MQ),
-                )
+            grouped = grouped_pool.tile(
+                [P, PARTS, PASSES, PART_MR * J, 2, MQ, PACK], BF16, tag="grouped_reply", align_bytes=64
+            )
+            width = PART_MR * J * MQ
+            for part in range(PARTS):
+                for twin in range(2):
+                    nc.scalar.copy(
+                        out=grouped[:, part, :, :, twin, :, :].bitcast(F32),
+                        in_=planes[:, :, part * width : (part + 1) * width].rearrange(
+                            "p (g u) (a q) -> p g a q u", u=2, q=MQ
+                        ),
+                    )
             return grouped
 
         def quantize_review(grouped):
@@ -224,30 +239,38 @@ def tile_positionwisedtableencoder_kernel(tc, review, reply, W_words, W_scales, 
             )
             return review_codes, review_planes
 
-        def quantize_reply(grouped):
-            reply_codes = packed.tile([P, PASSES * MR * J * 2 * MQ], I32, tag="reply_codes", align_bytes=64)
-            nc.vector.quantize_mx(
-                out=reply_codes[:].bitcast(FP8X4),
-                scales=reply_planes[:],
-                in_=grouped[:].rearrange("p g a r q t -> p (g a r q t)"),
-            )
-            return reply_codes
+        PART_WORDS = PASSES * PART_MR * J * 2 * MQ
 
-        def spread_reply(reply_codes):
-            spread_codes = packed.tile([P, PASSES, MR, P], I32, tag="spread_codes", align_bytes=64)
-            spread_planes = packed.tile([P, PASSES, MR, P], U8, tag="spread_planes", align_bytes=64)
+        def reply_tiles():
+            reply_codes = packed.tile([P, PARTS * PART_WORDS], I32, tag="reply_codes", align_bytes=64)
+            spread_codes = packed.tile([P, PARTS, PASSES, PART_MR, P], I32, tag="spread_codes", align_bytes=64)
+            spread_planes = packed.tile([P, PARTS, PASSES, PART_MR, P], U8, tag="spread_planes", align_bytes=64)
+            return reply_codes, spread_codes, spread_planes
+
+        def quantize_reply(grouped, tiles, part):
+            words = slice(part * PART_WORDS, (part + 1) * PART_WORDS)
+            nc.vector.quantize_mx(
+                out=tiles[0][:, words].bitcast(FP8X4),
+                scales=reply_planes[:, words],
+                in_=grouped[:, part].rearrange("p g a r q t -> p (g a r q t)"),
+            )
+
+        def spread_reply(tiles, part):
+            reply_codes, spread_codes, spread_planes = tiles
+            runs = PASSES * PART_MR * J
             nc.vector.tensor_copy(
-                out=spread_codes[:].rearrange("p g r (j a w) -> p (g r j) a w", a=NQ // 2, w=2 * MQ),
-                in_=reply_codes[:]
+                out=spread_codes[:, part].rearrange("p g r (j a w) -> p (g r j) a w", a=NQ // 2, w=2 * MQ),
+                in_=reply_codes[:, part * PART_WORDS : (part + 1) * PART_WORDS]
                 .rearrange("p (c w) -> p c w", w=2 * MQ)
                 .unsqueeze(2)
-                .to_broadcast([P, PASSES * MR * J, NQ // 2, 2 * MQ]),
+                .to_broadcast([P, runs, NQ // 2, 2 * MQ]),
             )
             nc.vector.tensor_copy(
-                out=spread_planes[:].bitcast(I32).rearrange("p g r (j a) -> p (g r j) a", a=NQ // 2),
-                in_=reply_planes[:].bitcast(I32).unsqueeze(2).to_broadcast([P, PASSES * MR * J, NQ // 2]),
+                out=spread_planes[:, part].bitcast(I32).rearrange("p g r (j a) -> p (g r j) a", a=NQ // 2),
+                in_=reply_planes[:].bitcast(I32)[:, part * runs : (part + 1) * runs]
+                .unsqueeze(2)
+                .to_broadcast([P, runs, NQ // 2]),
             )
-            return spread_codes, spread_planes
 
         def multiply(codes, planes, first_pass, h):
             cols = slice(h * N_TILE, (h + 1) * N_TILE)
@@ -274,10 +297,10 @@ def tile_positionwisedtableencoder_kernel(tc, review, reply, W_words, W_scales, 
 
         def multiply_reply(operands, bank):
             mr, h = bank // HALVES, bank % HALVES
-            spread_codes, spread_planes = operands
+            spread_codes, spread_planes = operands[1], operands[2]
             return multiply(
-                [spread_codes[:, g, mr, :] for g in range(PASSES)],
-                [spread_planes[:, g, mr, :] for g in range(PASSES)],
+                [spread_codes[:, mr // PART_MR, g, mr % PART_MR, :] for g in range(PASSES)],
+                [spread_planes[:, mr // PART_MR, g, mr % PART_MR, :] for g in range(PASSES)],
                 PASSES,
                 h,
             )
@@ -290,7 +313,7 @@ def tile_positionwisedtableencoder_kernel(tc, review, reply, W_words, W_scales, 
         gate = const.tile([P, 1], I32)
 
         def hold_gpsimd(spread_planes):
-            nc.gpsimd.tensor_copy(out=gate[:], in_=spread_planes[:, 0, 0, 0:4].bitcast(I32))
+            nc.gpsimd.tensor_copy(out=gate[:], in_=spread_planes[:, PARTS - 1, 0, 0, 0:4].bitcast(I32))
 
         out_rows = out.rearrange(
             "(g j) (nq nr) (mq mr) o -> g nr (j nq) mq (mr o)", j=J, nr=NR, mq=MQ
@@ -310,24 +333,27 @@ def tile_positionwisedtableencoder_kernel(tc, review, reply, W_words, W_scales, 
         def finish_preparation(group):
             review_sum = packed.tile([P, NR, OUT], F32, tag="review_sum")
             review_sums[group] = review_sum
+            tiles = reply_tiles()
+            reply_operands[group] = tiles
             early = 2 if group == 0 else 0
             for bank in range(early):
                 add_bias(review_sum, bank, review_accs[(group, bank)])
-            reply_codes = quantize_reply(grouped_reply[group])
-            for bank in range(early, REVIEW_BANKS - 2 + early // 2):
-                add_bias(review_sum, bank, review_accs[(group, bank)])
-            late = REVIEW_BANKS - 2 + early // 2
-            reply_operands[group] = spread_reply(reply_codes)
+            quantize_reply(grouped_reply[group], tiles, 0)
+            add_bias(review_sum, early, review_accs[(group, early)])
+            spread_reply(tiles, 0)
+            reply_accs[(group, 0)] = multiply_reply(tiles, 0)
+            reply_accs[(group, 1)] = multiply_reply(tiles, 1)
+            quantize_reply(grouped_reply[group], tiles, 1)
+            add_bias(review_sum, early + 1, review_accs[(group, early + 1)])
+            spread_reply(tiles, 1)
             if group + 1 < GROUPS:
-                hold_gpsimd(reply_operands[group][1])
+                hold_gpsimd(tiles[2])
                 y_review[group + 1] = rotate(nc.gpsimd, work_g, x_review[group + 1], "y_review%d" % (group + 1))
                 y_reply[group + 1] = rotate(nc.gpsimd, work_g, x_reply[group + 1], "y_reply%d" % (group + 1))
-            reply_accs[(group, 0)] = multiply_reply(reply_operands[group], 0)
-            reply_accs[(group, 1)] = multiply_reply(reply_operands[group], 1)
-            for bank in range(late, REVIEW_BANKS):
+            for bank in range(early + 2, REVIEW_BANKS):
                 add_bias(review_sum, bank, review_accs[(group, bank)])
-            reply_accs[(group, 2)] = multiply_reply(reply_operands[group], 2)
-            reply_accs[(group, 3)] = multiply_reply(reply_operands[group], 3)
+            reply_accs[(group, 2)] = multiply_reply(tiles, 2)
+            reply_accs[(group, 3)] = multiply_reply(tiles, 3)
 
         def table(group, steps):
             following = group + 1
@@ -343,10 +369,12 @@ def tile_positionwisedtableencoder_kernel(tc, review, reply, W_words, W_scales, 
                 cols = slice(h * N_TILE, (h + 1) * N_TILE)
                 if bank + LEAD < BANKS:
                     reply_accs[(group, bank + LEAD)] = multiply_reply(reply_operands[group], bank + LEAD)
-                elif following < GROUPS:
-                    review_accs[(following, bank + LEAD - BANKS)] = multiply_review(
-                        review_operands[following], bank + LEAD - BANKS
-                    )
+                if following < GROUPS and bank > QUANTIZE_AT:
+                    for review_bank in range(REVIEW_BANKS):
+                        if min(QUANTIZE_AT + 1 + review_bank, BANKS - 1) == bank:
+                            review_accs[(following, review_bank)] = multiply_review(
+                                review_operands[following], review_bank
+                            )
                 if following < GROUPS and bank == 7:
                     planes_review = transpose_words(y_review[following], order_review)
                 if following < GROUPS and bank == 11:
@@ -394,6 +422,7 @@ def tile_positionwisedtableencoder_kernel(tc, review, reply, W_words, W_scales, 
                     grouped_review[following] = copy_review(planes_review)
                 if following < GROUPS and bank == 11:
                     grouped_reply[following] = copy_reply(planes_reply)
+                if following < GROUPS and bank == QUANTIZE_AT:
                     review_operands[following] = quantize_review(grouped_review[following])
 
         y_review[0] = rotate(nc.vector, work_v, x_review[0], "y_review0")

@@ -31,7 +31,9 @@ WRAPPED = 128
 LOW = 32
 HIGH = PAIRS // LOW
 LEAD = 4
-QUANTIZE_AT = 12
+TURN_REVIEW_AT = 5
+TURN_REPLY_AT = 9
+QUANTIZE_AT = 10
 PARTS = 2
 PART_MR = MR // PARTS
 MAX_STEP = 1
@@ -46,7 +48,7 @@ def tile_positionwisedtableencoder_kernel(tc, review, reply, W_words, W_scales, 
         inputs = ctx.enter_context(tc.tile_pool(name="inputs", bufs=1))
         rotated = ctx.enter_context(tc.tile_pool(name="rotated", bufs=1))
         work_v = ctx.enter_context(tc.tile_pool(name="work_v", bufs=1))
-        work_g = ctx.enter_context(tc.tile_pool(name="work_g", bufs=1))
+        work_g = ctx.enter_context(tc.tile_pool(name="work_g", bufs=2))
         grouped_pool = ctx.enter_context(tc.tile_pool(name="grouped", bufs=2))
         packed = ctx.enter_context(tc.tile_pool(name="packed", bufs=2))
         stages = ctx.enter_context(tc.tile_pool(name="stages", bufs=10))
@@ -229,6 +231,38 @@ def tile_positionwisedtableencoder_kernel(tc, review, reply, W_words, W_scales, 
                     )
             return grouped
 
+        def transpose_sums(products, order):
+            straight, crossed = products
+            features = straight[:].rearrange("p i e -> p (i e)")
+            sums = [None] * PASSES
+            for g in range(PASSES):
+                planes = psum_t.tile([P, PACK, P], F32, tag="planes")
+                for t in range(PACK):
+                    u, e = t // 2, t % 2
+                    nc.tensor.matmul(
+                        planes[:, t, :], lhsT=features[:, K_PASS * g + t : K_PASS * (g + 1) : PACK], rhs=order,
+                        is_transpose=True, start=True, stop=False,
+                    )
+                    nc.tensor.matmul(
+                        planes[:, t, :], lhsT=crossed[:, e, 256 * g + u : 256 * (g + 1) : 2], rhs=order,
+                        is_transpose=True, start=False, stop=True,
+                    )
+                sums[g] = planes
+            return sums
+
+        def round_review(grouped, g, planes):
+            nc.scalar.copy(
+                out=grouped[:, g],
+                in_=planes[:].rearrange("p t c -> p c t").unsqueeze(2).to_broadcast([P, P, MQ, PACK]),
+            )
+
+        def round_reply(grouped, g, planes):
+            for twin in range(2):
+                nc.scalar.copy(
+                    out=grouped[:, :, g, :, twin, :, :],
+                    in_=planes[:].rearrange("p t (d a q) -> p d a q t", d=PARTS, q=MQ),
+                )
+
         def quantize_review(grouped):
             review_codes = packed.tile([P, PASSES * NR * P], I32, tag="review_codes", align_bytes=64)
             review_planes = packed.tile([P, PASSES * NR * P], U8, tag="review_planes", align_bytes=64)
@@ -348,8 +382,8 @@ def tile_positionwisedtableencoder_kernel(tc, review, reply, W_words, W_scales, 
             spread_reply(tiles, 1)
             if group + 1 < GROUPS:
                 hold_gpsimd(tiles[2])
-                y_review[group + 1] = rotate(nc.gpsimd, work_g, x_review[group + 1], "y_review%d" % (group + 1))
-                y_reply[group + 1] = rotate(nc.gpsimd, work_g, x_reply[group + 1], "y_reply%d" % (group + 1))
+                y_review[group + 1] = rotary_products(nc.gpsimd, work_g, x_review[group + 1])
+                y_reply[group + 1] = rotary_products(nc.gpsimd, work_g, x_reply[group + 1])
             for bank in range(early + 2, REVIEW_BANKS):
                 add_bias(review_sum, bank, review_accs[(group, bank)])
             reply_accs[(group, 2)] = multiply_reply(tiles, 2)
@@ -375,10 +409,10 @@ def tile_positionwisedtableencoder_kernel(tc, review, reply, W_words, W_scales, 
                             review_accs[(following, review_bank)] = multiply_review(
                                 review_operands[following], review_bank
                             )
-                if following < GROUPS and bank == 7:
-                    planes_review = transpose_words(y_review[following], order_review)
-                if following < GROUPS and bank == 11:
-                    planes_reply = transpose_words(y_reply[following], order_reply)
+                if following < GROUPS and bank == TURN_REVIEW_AT:
+                    planes_review = transpose_sums(y_review[following], order_review)
+                if following < GROUPS and bank == TURN_REPLY_AT:
+                    planes_reply = transpose_sums(y_reply[following], order_reply)
                 if h == 0 and mr in step_at:
                     stage = stages.tile([P, NR, MAX_STEP, OUT], F32, tag="stage")
                     first_mr = mr
@@ -418,10 +452,18 @@ def tile_positionwisedtableencoder_kernel(tc, review, reply, W_words, W_scales, 
                                 out=out_rows[group, nr][:, :, first_mr * OUT : (mr + 1) * OUT],
                                 in_=stage[:, nr, 0 : s + 1, :].rearrange("p s o -> p (s o)"),
                             )
-                if following < GROUPS and bank == 7:
-                    grouped_review[following] = copy_review(planes_review)
-                if following < GROUPS and bank == 11:
-                    grouped_reply[following] = copy_reply(planes_reply)
+                if following < GROUPS and bank == TURN_REVIEW_AT:
+                    rounded = grouped_pool.tile([P, PASSES, P, MQ, PACK], BF16, tag="grouped_review", align_bytes=64)
+                    for g in range(PASSES):
+                        round_review(rounded, g, planes_review[g])
+                    grouped_review[following] = rounded
+                if following < GROUPS and bank == TURN_REPLY_AT:
+                    rounded = grouped_pool.tile(
+                        [P, PARTS, PASSES, PART_MR * J, 2, MQ, PACK], BF16, tag="grouped_reply", align_bytes=64
+                    )
+                    for g in range(PASSES):
+                        round_reply(rounded, g, planes_reply[g])
+                    grouped_reply[following] = rounded
                 if following < GROUPS and bank == QUANTIZE_AT:
                     review_operands[following] = quantize_review(grouped_review[following])
 

@@ -231,24 +231,21 @@ def tile_positionwisedtableencoder_kernel(tc, review, reply, W_words, W_scales, 
                     )
             return grouped
 
-        def transpose_sums(products, order):
+        def transpose_sums(products, order, g):
             straight, crossed = products
             features = straight[:].rearrange("p i e -> p (i e)")
-            sums = [None] * PASSES
-            for g in range(PASSES):
-                planes = psum_t.tile([P, PACK, P], F32, tag="planes")
-                for t in range(PACK):
-                    u, e = t // 2, t % 2
-                    nc.tensor.matmul(
-                        planes[:, t, :], lhsT=features[:, K_PASS * g + t : K_PASS * (g + 1) : PACK], rhs=order,
-                        is_transpose=True, start=True, stop=False,
-                    )
-                    nc.tensor.matmul(
-                        planes[:, t, :], lhsT=crossed[:, e, 256 * g + u : 256 * (g + 1) : 2], rhs=order,
-                        is_transpose=True, start=False, stop=True,
-                    )
-                sums[g] = planes
-            return sums
+            planes = psum_t.tile([P, PACK, P], F32, tag="planes")
+            for t in range(PACK):
+                u, e = t // 2, t % 2
+                nc.tensor.matmul(
+                    planes[:, t, :], lhsT=features[:, K_PASS * g + t : K_PASS * (g + 1) : PACK], rhs=order,
+                    is_transpose=True, start=True, stop=False,
+                )
+                nc.tensor.matmul(
+                    planes[:, t, :], lhsT=crossed[:, e, 256 * g + u : 256 * (g + 1) : 2], rhs=order,
+                    is_transpose=True, start=False, stop=True,
+                )
+            return planes
 
         def round_review(grouped, g, planes):
             nc.scalar.copy(
@@ -409,10 +406,10 @@ def tile_positionwisedtableencoder_kernel(tc, review, reply, W_words, W_scales, 
                             review_accs[(following, review_bank)] = multiply_review(
                                 review_operands[following], review_bank
                             )
-                if following < GROUPS and bank == TURN_REVIEW_AT:
-                    planes_review = transpose_sums(y_review[following], order_review)
-                if following < GROUPS and bank == TURN_REPLY_AT:
-                    planes_reply = transpose_sums(y_reply[following], order_reply)
+                if following < GROUPS and 0 <= bank - TURN_REVIEW_AT < PASSES:
+                    planes_review = transpose_sums(y_review[following], order_review, bank - TURN_REVIEW_AT)
+                if following < GROUPS and 0 <= bank - TURN_REPLY_AT < PASSES:
+                    planes_reply = transpose_sums(y_reply[following], order_reply, bank - TURN_REPLY_AT)
                 if h == 0 and mr in step_at:
                     stage = stages.tile([P, NR, MAX_STEP, OUT], F32, tag="stage")
                     first_mr = mr
@@ -454,16 +451,16 @@ def tile_positionwisedtableencoder_kernel(tc, review, reply, W_words, W_scales, 
                             )
                 if following < GROUPS and bank == TURN_REVIEW_AT:
                     rounded = grouped_pool.tile([P, PASSES, P, MQ, PACK], BF16, tag="grouped_review", align_bytes=64)
-                    for g in range(PASSES):
-                        round_review(rounded, g, planes_review[g])
                     grouped_review[following] = rounded
+                if following < GROUPS and 0 <= bank - TURN_REVIEW_AT < PASSES:
+                    round_review(grouped_review[following], bank - TURN_REVIEW_AT, planes_review)
                 if following < GROUPS and bank == TURN_REPLY_AT:
                     rounded = grouped_pool.tile(
                         [P, PARTS, PASSES, PART_MR * J, 2, MQ, PACK], BF16, tag="grouped_reply", align_bytes=64
                     )
-                    for g in range(PASSES):
-                        round_reply(rounded, g, planes_reply[g])
                     grouped_reply[following] = rounded
+                if following < GROUPS and 0 <= bank - TURN_REPLY_AT < PASSES:
+                    round_reply(grouped_reply[following], bank - TURN_REPLY_AT, planes_reply)
                 if following < GROUPS and bank == QUANTIZE_AT:
                     review_operands[following] = quantize_review(grouped_review[following])
 

@@ -69,8 +69,6 @@ def tile_positionwisedtableencoder_kernel(tc, review, reply, W_words, W_scales, 
                 out=w_codes[:, g, :], in_=W_words[g].rearrange("p n t -> p (n t)").bitcast(I32)
             )
 
-        for g in range(PASSES):
-            load_codes(g)
 
         row_index = const.tile([P, 1], I32)
         nc.gpsimd.iota(row_index[:], pattern=[[0, 1]], base=0, channel_multiplier=1)
@@ -92,6 +90,8 @@ def tile_positionwisedtableencoder_kernel(tc, review, reply, W_words, W_scales, 
         high = const.tile([P, HIGH], F32)
         nc.vector.memset(low[:, 0:1], 1.0)
         nc.vector.memset(high[:, 0:1], 1.0)
+        position_int = const.tile([P, 1], I32)
+        position = const.tile([P, 1], F32)
         filled = 1
         while filled < LOW:
             nc.vector.tensor_scalar_mul(
@@ -103,11 +103,11 @@ def tile_positionwisedtableencoder_kernel(tc, review, reply, W_words, W_scales, 
                     in0=high[:, 0:filled],
                     scalar1=ROPE_BASE ** (-filled * LOW / PAIRS),
                 )
+            if filled == 2:
+                nc.vector.tensor_single_scalar(position_int[:], row_index[:], POSITIONS - 1, op=ALU.bitwise_and)
+            if filled == 8:
+                nc.vector.tensor_copy(out=position[:], in_=position_int[:])
             filled *= 2
-        position_int = const.tile([P, 1], I32)
-        nc.vector.tensor_single_scalar(position_int[:], row_index[:], POSITIONS - 1, op=ALU.bitwise_and)
-        position = const.tile([P, 1], F32)
-        nc.vector.tensor_copy(out=position[:], in_=position_int[:])
         angle = const.tile([P, PAIRS], F32)
         nc.vector.scalar_tensor_tensor(
             out=angle[:].rearrange("p (a b) -> p a b", b=LOW),
@@ -151,7 +151,7 @@ def tile_positionwisedtableencoder_kernel(tc, review, reply, W_words, W_scales, 
                 out=w_planes[32 * quadrant : 32 * quadrant + 16, :].bitcast(I32),
                 in_=W_scales[:, 4 * quadrant : 4 * quadrant + 4, :].bitcast(I32),
             )
-        for g in range(PASSES, 2 * PASSES):
+        for g in range(2 * PASSES):
             load_codes(g)
         for g in range(1, GROUPS):
             nc.sync.dma_start(out=x_review[g][:], in_=review_rows[g])

@@ -46,8 +46,7 @@ def tile_positionwisedtableencoder_kernel(tc, review, reply, W_words, W_scales, 
     with ExitStack() as ctx:
         const = ctx.enter_context(tc.tile_pool(name="const", bufs=1))
         inputs = ctx.enter_context(tc.tile_pool(name="inputs", bufs=1))
-        rotated = ctx.enter_context(tc.tile_pool(name="rotated", bufs=1))
-        work_v = ctx.enter_context(tc.tile_pool(name="work_v", bufs=1))
+        work_v = ctx.enter_context(tc.tile_pool(name="work_v", bufs=2))
         work_g = ctx.enter_context(tc.tile_pool(name="work_g", bufs=2))
         grouped_pool = ctx.enter_context(tc.tile_pool(name="grouped", bufs=2))
         packed = ctx.enter_context(tc.tile_pool(name="packed", bufs=2))
@@ -76,6 +75,8 @@ def tile_positionwisedtableencoder_kernel(tc, review, reply, W_words, W_scales, 
         nc.vector.memset(warm[:, 0:1], 0.0)
         nc.scalar.activation(out=warm[:, 1:2], in_=warm[:, 0:1], func=ACT.Sin)
 
+        bias_rows = const.tile([P, OUT], BF16)
+        nc.gpsimd.memset(bias_rows[:].bitcast(I32), 0)
         ones = const.tile([P, P], BF16)
         nc.gpsimd.memset(ones[:], 1.0)
         offsets = const.tile([P, 2, P], I32)
@@ -85,6 +86,10 @@ def tile_positionwisedtableencoder_kernel(tc, review, reply, W_words, W_scales, 
         nc.gpsimd.iota(
             offsets[:, 1, :], pattern=[[1, MR], [POSITIONS, J], [MR, MQ]], base=0, channel_multiplier=-1
         )
+
+        nc.sync.dma_start(out=bias_rows[0:1, :], in_=b.rearrange("(one o) -> one o", one=1))
+        for g in range(PASSES):
+            load_codes(g)
 
         low = const.tile([P, LOW], F32)
         high = const.tile([P, HIGH], F32)
@@ -136,46 +141,41 @@ def tile_positionwisedtableencoder_kernel(tc, review, reply, W_words, W_scales, 
         rest = slice(WRAPPED, PAIRS)
         nc.scalar.activation(out=trig[:, 0, rest], in_=angle[:, rest], func=ACT.Sin, bias=math.pi / 2)
         nc.scalar.activation(out=trig[:, 0, 0:WRAPPED], in_=wrapped[:, 0, :], func=ACT.Sin, bias=math.pi / 2)
-        nc.scalar.activation(out=trig[:, 1, rest], in_=angle[:, rest], func=ACT.Sin, scale=-1.0)
-        nc.scalar.activation(out=trig[:, 1, 0:WRAPPED], in_=wrapped[:, 1, :], func=ACT.Sin, scale=-1.0)
         nc.scalar.activation(out=trig[:, 2, rest], in_=angle[:, rest], func=ACT.Sin)
         nc.scalar.activation(out=trig[:, 2, 0:WRAPPED], in_=wrapped[:, 1, :], func=ACT.Sin)
-
-        bias_rows = const.tile([P, OUT], BF16)
-        nc.vector.memset(bias_rows[:], 0.0)
-        nc.sync.dma_start(out=bias_rows[0:1, :], in_=b.rearrange("(one o) -> one o", one=1))
-        w_planes = const.tile([P, OUT], U8, align_bytes=64)
-        nc.vector.memset(w_planes[:].bitcast(I32), 0)
-        for quadrant in range(4):
-            nc.sync.dma_start(
-                out=w_planes[32 * quadrant : 32 * quadrant + 16, :].bitcast(I32),
-                in_=W_scales[:, 4 * quadrant : 4 * quadrant + 4, :].bitcast(I32),
-            )
-        for g in range(2 * PASSES):
-            load_codes(g)
-        for g in range(1, GROUPS):
-            nc.sync.dma_start(out=x_review[g][:], in_=review_rows[g])
-            nc.sync.dma_start(out=x_reply[g][:], in_=reply_rows[g])
-
-        orders = const.tile([P, 2, P], F32)
-        nc.vector.tensor_single_scalar(orders[:], offsets[:], 0, op=ALU.is_equal)
-        order_review = orders[:, 0, :]
-        order_reply = orders[:, 1, :]
-
-        reply_planes = const.tile([P, PASSES * MR * J * 2 * MQ], U8, align_bytes=64)
-        nc.vector.memset(reply_planes[:].bitcast(I32), 0)
-
         bias_all = const.tile([P, OUT], F32)
         for h in range(HALVES):
             cols = slice(h * N_TILE, (h + 1) * N_TILE)
             spread = psum_acc.tile([P, N_TILE], F32, tag="acc")
             nc.tensor.matmul(spread[:], lhsT=ones[:], rhs=bias_rows[:, cols], start=True, stop=True)
             nc.scalar.copy(out=bias_all[:, cols], in_=spread[:])
+        nc.scalar.activation(out=trig[:, 1, rest], in_=angle[:, rest], func=ACT.Sin, scale=-1.0)
+        nc.scalar.activation(out=trig[:, 1, 0:WRAPPED], in_=wrapped[:, 1, :], func=ACT.Sin, scale=-1.0)
 
-        def rotary_products(engine, pool, x):
+        orders = const.tile([P, 2, P], F32)
+        nc.vector.tensor_single_scalar(orders[:], offsets[:], 0, op=ALU.is_equal)
+        order_review = orders[:, 0, :]
+        order_reply = orders[:, 1, :]
+        w_planes = const.tile([P, OUT], U8, align_bytes=64)
+        nc.vector.memset(w_planes[:].bitcast(I32), 0)
+        reply_planes = const.tile([P, PASSES * MR * J * 2 * MQ], U8, align_bytes=64)
+        nc.vector.memset(reply_planes[:].bitcast(I32), 0)
+        for quadrant in range(4):
+            nc.sync.dma_start(
+                out=w_planes[32 * quadrant : 32 * quadrant + 16, :].bitcast(I32),
+                in_=W_scales[:, 4 * quadrant : 4 * quadrant + 4, :].bitcast(I32),
+            )
+        for g in range(PASSES, 2 * PASSES):
+            load_codes(g)
+        for g in range(1, GROUPS):
+            nc.sync.dma_start(out=x_review[g][:], in_=review_rows[g])
+            nc.sync.dma_start(out=x_reply[g][:], in_=reply_rows[g])
+
+        def rotary_products(x):
+            engine = nc.gpsimd
             pairs = x[:].rearrange("p (i e) -> p i e", e=2)
-            straight = pool.tile([P, PAIRS, 2], F32, tag="straight")
-            crossed = pool.tile([P, 2, PAIRS], F32, tag="crossed")
+            straight = work_g.tile([P, PAIRS, 2], F32, tag="straight")
+            crossed = work_g.tile([P, 2, PAIRS], F32, tag="crossed")
             engine.tensor_tensor(
                 out=straight[:], in0=pairs, in1=cos.unsqueeze(2).to_broadcast([P, PAIRS, 2]), op=ALU.mult
             )
@@ -183,53 +183,44 @@ def tile_positionwisedtableencoder_kernel(tc, review, reply, W_words, W_scales, 
             engine.tensor_tensor(out=crossed[:, 1, :], in0=pairs[:, :, 0], in1=sin, op=ALU.mult)
             return straight, crossed
 
-        def rotary_sum(engine, products, name):
+        halves = [slice(g * PAIRS // PASSES, (g + 1) * PAIRS // PASSES) for g in range(PASSES)]
+
+        def straight_product_vector(tiles, x, g):
+            nc.vector.tensor_tensor(
+                out=tiles[0][:, g * K_PASS : (g + 1) * K_PASS].rearrange("p (u e i) -> p u e i", u=2, e=2),
+                in0=x[:, g * K_PASS : (g + 1) * K_PASS].rearrange("p (i u e) -> p u e i", u=2, e=2),
+                in1=cos[:, halves[g]].rearrange("p (i u) -> p u i", u=2).unsqueeze(2).to_broadcast([P, 2, 2, P]),
+                op=ALU.mult,
+            )
+
+        def crossed_products_vector(tiles, x, g):
+            features = x[:, g * K_PASS : (g + 1) * K_PASS].rearrange("p (i u e) -> p e u i", u=2, e=2)
+            sine = sin[:, halves[g]].rearrange("p (i u) -> p u i", u=2)
+            planes = tiles[1][:, g].rearrange("p e (u i) -> p e u i", u=2)
+            nc.vector.tensor_tensor(out=planes[:, 1], in0=features[:, 0], in1=sine, op=ALU.mult)
+            nc.vector.scalar_tensor_tensor(
+                out=planes[:, 0], in0=features[:, 1], scalar=-1.0, in1=sine, op0=ALU.mult, op1=ALU.mult
+            )
+
+        def product_tiles_vector():
+            straight = work_v.tile([P, FEATURES], F32, tag="straight")
+            crossed = work_v.tile([P, PASSES, 2, PAIRS // PASSES], F32, tag="crossed")
+            return straight, crossed
+
+        def transpose_planes(products, order, g, pool, tag):
             straight, crossed = products
-            y = rotated.tile([P, PAIRS, 2], BF16, name=name)
-            engine.tensor_tensor(
-                out=y[:], in0=straight[:], in1=crossed[:].rearrange("p e i -> p i e"), op=ALU.add
-            )
-            return y
-
-        def rotate(engine, pool, x, name):
-            return rotary_sum(engine, rotary_products(engine, pool, x), name)
-
-        def transpose_words(y, order):
-            words = y[:].rearrange("p i e -> p (i e)").bitcast(F32)
-            planes = psum_t.tile([P, PASSES * 2, P], F32, tag="planes")
-            for g in range(PASSES):
-                for u in range(2):
-                    nc.tensor.transpose(
-                        planes[:, 2 * g + u, :], words[:, 256 * g + u : 256 * (g + 1) : 2], order
-                    )
-            return planes
-
-        def copy_review(planes):
-            grouped = grouped_pool.tile([P, PASSES, P, MQ, PACK], BF16, tag="grouped_review", align_bytes=64)
-            for g in range(PASSES):
-                nc.scalar.copy(
-                    out=grouped[:, g].bitcast(F32),
-                    in_=planes[:, 2 * g : 2 * g + 2, :]
-                    .rearrange("p u c -> p c u")
-                    .unsqueeze(2)
-                    .to_broadcast([P, P, MQ, 2]),
+            planes = pool.tile([P, PACK, P], F32, tag=tag)
+            for t in range(PACK):
+                u, e = t // 2, t % 2
+                nc.tensor.matmul(
+                    planes[:, t, :], lhsT=straight[:, K_PASS * g + t * P : K_PASS * g + (t + 1) * P], rhs=order,
+                    is_transpose=True, start=True, stop=False,
                 )
-            return grouped
-
-        def copy_reply(planes):
-            grouped = grouped_pool.tile(
-                [P, PARTS, PASSES, PART_MR * J, 2, MQ, PACK], BF16, tag="grouped_reply", align_bytes=64
-            )
-            width = PART_MR * J * MQ
-            for part in range(PARTS):
-                for twin in range(2):
-                    nc.scalar.copy(
-                        out=grouped[:, part, :, :, twin, :, :].bitcast(F32),
-                        in_=planes[:, :, part * width : (part + 1) * width].rearrange(
-                            "p (g u) (a q) -> p g a q u", u=2, q=MQ
-                        ),
-                    )
-            return grouped
+                nc.tensor.matmul(
+                    planes[:, t, :], lhsT=crossed[:, g, e, u * P : (u + 1) * P], rhs=order,
+                    is_transpose=True, start=False, stop=True,
+                )
+            return planes
 
         def transpose_sums(products, order, g):
             straight, crossed = products
@@ -247,8 +238,8 @@ def tile_positionwisedtableencoder_kernel(tc, review, reply, W_words, W_scales, 
                 )
             return planes
 
-        def round_review(grouped, g, planes):
-            nc.scalar.copy(
+        def round_review(copy, grouped, g, planes):
+            copy(
                 out=grouped[:, g],
                 in_=planes[:].rearrange("p t c -> p c t").unsqueeze(2).to_broadcast([P, P, MQ, PACK]),
             )
@@ -259,6 +250,16 @@ def tile_positionwisedtableencoder_kernel(tc, review, reply, W_words, W_scales, 
                     out=grouped[:, :, g, :, twin, :, :],
                     in_=planes[:].rearrange("p t (d a q) -> p d a q t", d=PARTS, q=MQ),
                 )
+
+        def round_reply_part(grouped, g, planes, part):
+            width = PART_MR * J * MQ
+            nc.scalar.copy(
+                out=grouped[:, part, g],
+                in_=planes[:, :, part * width : (part + 1) * width]
+                .rearrange("p t (a q) -> p a q t", q=MQ)
+                .unsqueeze(2)
+                .to_broadcast([P, PART_MR * J, 2, MQ, PACK]),
+            )
 
         def quantize_review(grouped):
             review_codes = packed.tile([P, PASSES * NR * P], I32, tag="review_codes", align_bytes=64)
@@ -366,22 +367,19 @@ def tile_positionwisedtableencoder_kernel(tc, review, reply, W_words, W_scales, 
             review_sums[group] = review_sum
             tiles = reply_tiles()
             reply_operands[group] = tiles
-            early = 2 if group == 0 else 0
-            for bank in range(early):
-                add_bias(review_sum, bank, review_accs[(group, bank)])
             quantize_reply(grouped_reply[group], tiles, 0)
-            add_bias(review_sum, early, review_accs[(group, early)])
+            add_bias(review_sum, 0, review_accs[(group, 0)])
             spread_reply(tiles, 0)
             reply_accs[(group, 0)] = multiply_reply(tiles, 0)
             reply_accs[(group, 1)] = multiply_reply(tiles, 1)
             quantize_reply(grouped_reply[group], tiles, 1)
-            add_bias(review_sum, early + 1, review_accs[(group, early + 1)])
+            add_bias(review_sum, 1, review_accs[(group, 1)])
             spread_reply(tiles, 1)
             if group + 1 < GROUPS:
                 hold_gpsimd(tiles[2])
-                y_review[group + 1] = rotary_products(nc.gpsimd, work_g, x_review[group + 1])
-                y_reply[group + 1] = rotary_products(nc.gpsimd, work_g, x_reply[group + 1])
-            for bank in range(early + 2, REVIEW_BANKS):
+                y_review[group + 1] = rotary_products(x_review[group + 1])
+                y_reply[group + 1] = rotary_products(x_reply[group + 1])
+            for bank in range(2, REVIEW_BANKS):
                 add_bias(review_sum, bank, review_accs[(group, bank)])
             reply_accs[(group, 2)] = multiply_reply(tiles, 2)
             reply_accs[(group, 3)] = multiply_reply(tiles, 3)
@@ -453,7 +451,7 @@ def tile_positionwisedtableencoder_kernel(tc, review, reply, W_words, W_scales, 
                     rounded = grouped_pool.tile([P, PASSES, P, MQ, PACK], BF16, tag="grouped_review", align_bytes=64)
                     grouped_review[following] = rounded
                 if following < GROUPS and 0 <= bank - TURN_REVIEW_AT < PASSES:
-                    round_review(grouped_review[following], bank - TURN_REVIEW_AT, planes_review)
+                    round_review(nc.scalar.copy, grouped_review[following], bank - TURN_REVIEW_AT, planes_review)
                 if following < GROUPS and bank == TURN_REPLY_AT:
                     rounded = grouped_pool.tile(
                         [P, PARTS, PASSES, PART_MR * J, 2, MQ, PACK], BF16, tag="grouped_reply", align_bytes=64
@@ -464,15 +462,28 @@ def tile_positionwisedtableencoder_kernel(tc, review, reply, W_words, W_scales, 
                 if following < GROUPS and bank == QUANTIZE_AT:
                     review_operands[following] = quantize_review(grouped_review[following])
 
-        y_review[0] = rotate(nc.vector, work_v, x_review[0], "y_review0")
-        grouped_review[0] = copy_review(transpose_words(y_review[0], order_review))
-        products = rotary_products(nc.vector, work_v, x_reply[0])
-        review_operands[0] = quantize_review(grouped_review[0])
-        for bank in range(REVIEW_BANKS // 2):
-            review_accs[(0, bank)] = multiply_review(review_operands[0], bank)
-        y_reply[0] = rotary_sum(nc.vector, products, "y_reply0")
-        grouped_reply[0] = copy_reply(transpose_words(y_reply[0], order_reply))
-        for bank in range(REVIEW_BANKS // 2, REVIEW_BANKS):
+        first_review = product_tiles_vector()
+        first_reply = product_tiles_vector()
+        for g in range(PASSES):
+            straight_product_vector(first_review, x_review[0], g)
+        for g in range(PASSES):
+            crossed_products_vector(first_review, x_review[0], g)
+        for g in range(PASSES):
+            straight_product_vector(first_reply, x_reply[0], g)
+            crossed_products_vector(first_reply, x_reply[0], g)
+        rounded = grouped_pool.tile([P, PASSES, P, MQ, PACK], BF16, tag="grouped_review", align_bytes=64)
+        for g, copy in enumerate((nc.scalar.copy, nc.vector.tensor_copy)):
+            round_review(copy, rounded, g, transpose_planes(first_review, order_review, g, psum_t, "planes"))
+        review_operands[0] = quantize_review(rounded)
+        planes_reply = [transpose_planes(first_reply, order_reply, g, psum_acc, "acc") for g in range(PASSES)]
+        rounded = grouped_pool.tile(
+            [P, PARTS, PASSES, PART_MR * J, 2, MQ, PACK], BF16, tag="grouped_reply", align_bytes=64
+        )
+        grouped_reply[0] = rounded
+        for part in range(PARTS):
+            for g in range(PASSES):
+                round_reply_part(rounded, g, planes_reply[g], part)
+        for bank in range(REVIEW_BANKS):
             review_accs[(0, bank)] = multiply_review(review_operands[0], bank)
         for group in range(GROUPS):
             finish_preparation(group)

@@ -34,6 +34,7 @@ LEAD = 4
 TURN_REVIEW_AT = 5
 TURN_REPLY_AT = 9
 QUANTIZE_AT = 10
+WARM_UPS = 4
 PARTS = 2
 PART_MR = MR // PARTS
 MAX_STEP = 1
@@ -79,6 +80,12 @@ def tile_positionwisedtableencoder_kernel(tc, review, reply, W_words, W_scales, 
         nc.gpsimd.memset(bias_rows[:].bitcast(I32), 0)
         ones = const.tile([P, P], BF16)
         nc.gpsimd.memset(ones[:], 1.0)
+        warm_bank = psum_acc.tile([P, N_TILE], F32, tag="acc")
+        for step in range(WARM_UPS):
+            nc.tensor.matmul(
+                warm_bank[:], lhsT=ones[:], rhs=ones[:].unsqueeze(1).to_broadcast([P, N_TILE // P, P]),
+                start=True, stop=True,
+            )
         offsets = const.tile([P, 2, P], I32)
         nc.gpsimd.iota(
             offsets[:, 0, :], pattern=[[1, NR], [POSITIONS, J], [NR, NQ]], base=0, channel_multiplier=-1
@@ -207,6 +214,11 @@ def tile_positionwisedtableencoder_kernel(tc, review, reply, W_words, W_scales, 
             crossed = work_v.tile([P, PASSES, 2, PAIRS // PASSES], F32, tag="crossed")
             return straight, crossed
 
+        def keep_warm(products):
+            nc.tensor.matmul(
+                warm_bank[:, 0 : 2 * P], lhsT=order_review, rhs=products[0][:, 0 : 2 * P], start=True, stop=True
+            )
+
         def transpose_planes(products, order, g, pool, tag):
             straight, crossed = products
             planes = pool.tile([P, PACK, P], F32, tag=tag)
@@ -238,8 +250,8 @@ def tile_positionwisedtableencoder_kernel(tc, review, reply, W_words, W_scales, 
                 )
             return planes
 
-        def round_review(copy, grouped, g, planes):
-            copy(
+        def round_review(grouped, g, planes):
+            nc.scalar.copy(
                 out=grouped[:, g],
                 in_=planes[:].rearrange("p t c -> p c t").unsqueeze(2).to_broadcast([P, P, MQ, PACK]),
             )
@@ -412,14 +424,33 @@ def tile_positionwisedtableencoder_kernel(tc, review, reply, W_words, W_scales, 
                     stage = stages.tile([P, NR, MAX_STEP, OUT], F32, tag="stage")
                     first_mr = mr
                 s = mr - first_mr
+                if group == GROUPS - 1 and bank == BANKS - 1:
+                    middle = h * N_TILE + N_TILE // 2
+                    for nr in range(NR):
+                        nc.vector.tensor_tensor(
+                            out=stage[:, nr, s, cols],
+                            in0=reply_accs[(group, bank)][:],
+                            in1=review_sums[group][:, nr, cols],
+                            op=ALU.add,
+                        )
+                        early, late = stage[:, nr, s, cols.start : middle], stage[:, nr, s, middle : cols.stop]
+                        nc.scalar.activation(out=early, in_=early, func=ACT.Relu)
+                        nc.gpsimd.tensor_scalar(
+                            out=late, in0=late, scalar1=float("inf"), scalar2=0.0, op0=ALU.min, op1=ALU.max
+                        )
+                        nc.sync.dma_start(
+                            out=out_rows[group, nr][:, :, mr * OUT + cols.start : mr * OUT + cols.stop],
+                            in_=stage[:, nr, s, cols],
+                        )
+                    continue
                 nc.vector.tensor_tensor(
                     out=stage[:, :, s, cols],
                     in0=reply_accs[(group, bank)][:].unsqueeze(1).to_broadcast([P, NR, N_TILE]),
                     in1=review_sums[group][:, :, cols],
                     op=ALU.add,
                 )
-                if group == GROUPS - 1 and mr == MR - 1:
-                    if h < HALVES - 1:
+                if (group == GROUPS - 1 and mr >= MR - 2) or (group == 0 and mr == 0):
+                    if group == 0:
                         nc.scalar.activation(out=stage[:, :, s, cols], in_=stage[:, :, s, cols], func=ACT.Relu)
                     else:
                         nc.scalar.activation(out=stage[:, 0, s, cols], in_=stage[:, 0, s, cols], func=ACT.Relu)
@@ -429,7 +460,7 @@ def tile_positionwisedtableencoder_kernel(tc, review, reply, W_words, W_scales, 
                         )
                     for nr in range(NR):
                         nc.sync.dma_start(
-                            out=out_rows[group, nr][:, :, mr * OUT + h * N_TILE : mr * OUT + (h + 1) * N_TILE],
+                            out=out_rows[group, nr][:, :, mr * OUT + cols.start : mr * OUT + cols.stop],
                             in_=stage[:, nr, s, cols],
                         )
                 elif h == HALVES - 1:
@@ -451,7 +482,7 @@ def tile_positionwisedtableencoder_kernel(tc, review, reply, W_words, W_scales, 
                     rounded = grouped_pool.tile([P, PASSES, P, MQ, PACK], BF16, tag="grouped_review", align_bytes=64)
                     grouped_review[following] = rounded
                 if following < GROUPS and 0 <= bank - TURN_REVIEW_AT < PASSES:
-                    round_review(nc.scalar.copy, grouped_review[following], bank - TURN_REVIEW_AT, planes_review)
+                    round_review(grouped_review[following], bank - TURN_REVIEW_AT, planes_review)
                 if following < GROUPS and bank == TURN_REPLY_AT:
                     rounded = grouped_pool.tile(
                         [P, PARTS, PASSES, PART_MR * J, 2, MQ, PACK], BF16, tag="grouped_reply", align_bytes=64
@@ -472,10 +503,14 @@ def tile_positionwisedtableencoder_kernel(tc, review, reply, W_words, W_scales, 
             straight_product_vector(first_reply, x_reply[0], g)
             crossed_products_vector(first_reply, x_reply[0], g)
         rounded = grouped_pool.tile([P, PASSES, P, MQ, PACK], BF16, tag="grouped_review", align_bytes=64)
-        for g, copy in enumerate((nc.scalar.copy, nc.vector.tensor_copy)):
-            round_review(copy, rounded, g, transpose_planes(first_review, order_review, g, psum_t, "planes"))
+        keep_warm(first_review)
+        for g in range(PASSES):
+            round_review(rounded, g, transpose_planes(first_review, order_review, g, psum_t, "planes"))
         review_operands[0] = quantize_review(rounded)
-        planes_reply = [transpose_planes(first_reply, order_reply, g, psum_acc, "acc") for g in range(PASSES)]
+        planes_reply = []
+        for g in range(PASSES):
+            keep_warm(first_review)
+            planes_reply.append(transpose_planes(first_reply, order_reply, g, psum_acc, "acc"))
         rounded = grouped_pool.tile(
             [P, PARTS, PASSES, PART_MR * J, 2, MQ, PACK], BF16, tag="grouped_reply", align_bytes=64
         )

@@ -35,6 +35,7 @@ TURN_REVIEW_AT = 5
 TURN_REPLY_AT = 9
 QUANTIZE_AT = 10
 WARM_UPS = 4
+GPSIMD_RELU = 5
 PARTS = 2
 PART_MR = MR // PARTS
 MAX_STEP = 1
@@ -379,19 +380,20 @@ def tile_positionwisedtableencoder_kernel(tc, review, reply, W_words, W_scales, 
             review_sums[group] = review_sum
             tiles = reply_tiles()
             reply_operands[group] = tiles
+            order = (0, HALVES) if group == 0 else range(REVIEW_BANKS)
             quantize_reply(grouped_reply[group], tiles, 0)
-            add_bias(review_sum, 0, review_accs[(group, 0)])
+            add_bias(review_sum, order[0], review_accs[(group, order[0])])
             spread_reply(tiles, 0)
             reply_accs[(group, 0)] = multiply_reply(tiles, 0)
             reply_accs[(group, 1)] = multiply_reply(tiles, 1)
             quantize_reply(grouped_reply[group], tiles, 1)
-            add_bias(review_sum, 1, review_accs[(group, 1)])
+            add_bias(review_sum, order[1], review_accs[(group, order[1])])
             spread_reply(tiles, 1)
             if group + 1 < GROUPS:
                 hold_gpsimd(tiles[2])
                 y_review[group + 1] = rotary_products(x_review[group + 1])
                 y_reply[group + 1] = rotary_products(x_reply[group + 1])
-            for bank in range(2, REVIEW_BANKS):
+            for bank in order[2:]:
                 add_bias(review_sum, bank, review_accs[(group, bank)])
             reply_accs[(group, 2)] = multiply_reply(tiles, 2)
             reply_accs[(group, 3)] = multiply_reply(tiles, 3)
@@ -408,7 +410,11 @@ def tile_positionwisedtableencoder_kernel(tc, review, reply, W_words, W_scales, 
             for bank in range(BANKS):
                 mr, h = bank // HALVES, bank % HALVES
                 cols = slice(h * N_TILE, (h + 1) * N_TILE)
-                if bank + LEAD < BANKS:
+                if group == 0 and bank == 1:
+                    for review_bank in range(1, REVIEW_BANKS, HALVES):
+                        add_bias(review_sums[0], review_bank, review_accs[(0, review_bank)])
+                    reply_accs[(0, LEAD)] = multiply_reply(reply_operands[0], LEAD)
+                if (group > 0 or bank > 0) and bank + LEAD < BANKS:
                     reply_accs[(group, bank + LEAD)] = multiply_reply(reply_operands[group], bank + LEAD)
                 if following < GROUPS and bank > QUANTIZE_AT:
                     for review_bank in range(REVIEW_BANKS):
@@ -470,6 +476,11 @@ def tile_positionwisedtableencoder_kernel(tc, review, reply, W_words, W_scales, 
                             out=stage[:, 1, s, :], in0=stage[:, 1, s, :],
                             scalar1=float("inf"), scalar2=0.0, op0=ALU.min, op1=ALU.max,
                         )
+                    elif mr == GPSIMD_RELU:
+                        nc.gpsimd.tensor_scalar(
+                            out=stage[:, :, s, :], in0=stage[:, :, s, :],
+                            scalar1=float("inf"), scalar2=0.0, op0=ALU.min, op1=ALU.max,
+                        )
                     else:
                         nc.scalar.activation(out=stage[:, :, s, :], in_=stage[:, :, s, :], func=ACT.Relu)
                     if s == step_at[first_mr] - 1:
@@ -518,8 +529,9 @@ def tile_positionwisedtableencoder_kernel(tc, review, reply, W_words, W_scales, 
         for part in range(PARTS):
             for g in range(PASSES):
                 round_reply_part(rounded, g, planes_reply[g], part)
-        for bank in range(REVIEW_BANKS):
-            review_accs[(0, bank)] = multiply_review(review_operands[0], bank)
+        for h in range(HALVES):
+            for bank in range(h, REVIEW_BANKS, HALVES):
+                review_accs[(0, bank)] = multiply_review(review_operands[0], bank)
         for group in range(GROUPS):
             finish_preparation(group)
             table(group, [1] * 8)

from contextlib import ExitStack
import math

import concourse.mybir as mybir

F32 = mybir.dt.float32
BF16 = mybir.dt.bfloat16
I32 = mybir.dt.int32
U8 = mybir.dt.uint8
FP8X4 = mybir.dt.float8_e4m3fn_x4
ALU = mybir.AluOpType
ACT = mybir.ActivationFunctionType

P = 128
BATCH = 24
POSITIONS = 16
FEATURES = 1024
PAIRS = FEATURES // 2
OUT = 1024
PACK = 4
K_PASS = P * PACK
PASSES = FEATURES // K_PASS
N_TILE = 512
HALVES = OUT // N_TILE
J = P // POSITIONS
GROUPS = BATCH // J
NQ, NR = 8, 2
MQ, MR = 2, 8
ROPE_BASE = 10000.0
WRAPPED = 128
LOW = 32
HIGH = PAIRS // LOW
LEAD = 4
TURN_REVIEW_AT = 5
TURN_REPLY_AT = 9
QUANTIZE_AT = 10
WARM_UPS = 4
GPSIMD_RELU = 5
PARTS = 2
PART_MR = MR // PARTS
MAX_STEP = 1

FLOPS = 2 * 2 * BATCH * POSITIONS * FEATURES * OUT


def tile_positionwisedtableencoder_kernel(tc, review, reply, W_words, W_scales, b, out):
    nc = tc.nc
    with ExitStack() as ctx:
        const = ctx.enter_context(tc.tile_pool(name="const", bufs=1))
        inputs = ctx.enter_context(tc.tile_pool(name="inputs", bufs=1))
        work_v = ctx.enter_context(tc.tile_pool(name="work_v", bufs=2))
        work_g = ctx.enter_context(tc.tile_pool(name="work_g", bufs=2))
        grouped_pool = ctx.enter_context(tc.tile_pool(name="grouped", bufs=2))
        packed = ctx.enter_context(tc.tile_pool(name="packed", bufs=2))
        stages = ctx.enter_context(tc.tile_pool(name="stages", bufs=10))
        psum_t = ctx.enter_context(tc.psum_pool(name="psum_t", bufs=2))
        psum_acc = ctx.enter_context(tc.psum_pool(name="psum_acc", bufs=6))
        ctx.enter_context(tc.manual_schedule())

        review_rows = review.rearrange("(g j) n h -> g (j n) h", j=J)
        reply_rows = reply.rearrange("(g j) m h -> g (j m) h", j=J)
        x_review = [inputs.tile([P, FEATURES], BF16, name="x_review%d" % g) for g in range(GROUPS)]
        x_reply = [inputs.tile([P, FEATURES], BF16, name="x_reply%d" % g) for g in range(GROUPS)]
        nc.scalar.dma_start(out=x_review[0][:], in_=review_rows[0])
        nc.sync.dma_start(out=x_reply[0][:], in_=reply_rows[0])
        w_codes = const.tile([P, 2 * PASSES, OUT], I32, align_bytes=64)

        def load_codes(g):
            nc.sync.dma_start(
                out=w_codes[:, g, :], in_=W_words[g].rearrange("p n t -> p (n t)").bitcast(I32)
            )


        row_index = const.tile([P, 1], I32)
        nc.gpsimd.iota(row_index[:], pattern=[[0, 1]], base=0, channel_multiplier=1)
        warm = const.tile([P, 2], F32)
        nc.vector.memset(warm[:, 0:1], 0.0)
        nc.scalar.activation(out=warm[:, 1:2], in_=warm[:, 0:1], func=ACT.Sin)

        bias_rows = const.tile([P, OUT], BF16)
        nc.gpsimd.memset(bias_rows[:].bitcast(I32), 0)
        ones = const.tile([P, P], BF16)
        nc.gpsimd.memset(ones[:], 1.0)
        warm_bank = psum_acc.tile([P, N_TILE], F32, tag="acc")
        for step in range(WARM_UPS):
            nc.tensor.matmul(
                warm_bank[:], lhsT=ones[:], rhs=ones[:].unsqueeze(1).to_broadcast([P, N_TILE // P, P]),
                start=True, stop=True,
            )
        offsets = const.tile([P, 2, P], I32)
        nc.gpsimd.iota(
            offsets[:, 0, :], pattern=[[1, NR], [POSITIONS, J], [NR, NQ]], base=0, channel_multiplier=-1
        )
        nc.gpsimd.iota(
            offsets[:, 1, :], pattern=[[1, MR], [POSITIONS, J], [MR, MQ]], base=0, channel_multiplier=-1
        )

        nc.sync.dma_start(out=bias_rows[0:1, :], in_=b.rearrange("(one o) -> one o", one=1))
        for g in range(PASSES):
            load_codes(g)

        low = const.tile([P, LOW], F32)
        high = const.tile([P, HIGH], F32)
        nc.vector.memset(low[:, 0:1], 1.0)
        nc.vector.memset(high[:, 0:1], 1.0)
        position_int = const.tile([P, 1], I32)
        position = const.tile([P, 1], F32)
        filled = 1
        while filled < LOW:
            nc.vector.tensor_scalar_mul(
                out=low[:, filled : 2 * filled], in0=low[:, 0:filled], scalar1=ROPE_BASE ** (-filled / PAIRS)
            )
            if filled < HIGH:
                nc.vector.tensor_scalar_mul(
                    out=high[:, filled : 2 * filled],
                    in0=high[:, 0:filled],
                    scalar1=ROPE_BASE ** (-filled * LOW / PAIRS),
                )
            if filled == 2:
                nc.vector.tensor_single_scalar(position_int[:], row_index[:], POSITIONS - 1, op=ALU.bitwise_and)
            if filled == 8:
                nc.vector.tensor_copy(out=position[:], in_=position_int[:])
            filled *= 2
        angle = const.tile([P, PAIRS], F32)
        nc.vector.scalar_tensor_tensor(
            out=angle[:].rearrange("p (a b) -> p a b", b=LOW),
            in0=high[:].unsqueeze(2).to_broadcast([P, HIGH, LOW]),
            scalar=position[:, 0:1],
            in1=low[:].unsqueeze(1).to_broadcast([P, HIGH, LOW]),
            op0=ALU.mult,
            op1=ALU.mult,
        )
        turns = const.tile([P, 2, WRAPPED], I32)
        nc.vector.tensor_scalar(
            out=turns[:, 0, :], in0=angle[:, 0:WRAPPED], scalar1=1.0 / (2.0 * math.pi), scalar2=0.25,
            op0=ALU.mult, op1=ALU.add,
        )
        nc.vector.tensor_scalar_mul(out=turns[:, 1, :], in0=angle[:, 0:WRAPPED], scalar1=1.0 / (2.0 * math.pi))
        wrapped = const.tile([P, 2, WRAPPED], F32)
        for plane in range(2):
            nc.vector.scalar_tensor_tensor(
                out=wrapped[:, plane, :], in0=turns[:, plane, :], scalar=-2.0 * math.pi, in1=angle[:, 0:WRAPPED],
                op0=ALU.mult, op1=ALU.add,
            )
        trig = const.tile([P, 3, PAIRS], F32)
        cos = trig[:, 0, :]
        minus_sin = trig[:, 1, :]
        sin = trig[:, 2, :]
        rest = slice(WRAPPED, PAIRS)
        nc.scalar.activation(out=trig[:, 0, rest], in_=angle[:, rest], func=ACT.Sin, bias=math.pi / 2)
        nc.scalar.activation(out=trig[:, 0, 0:WRAPPED], in_=wrapped[:, 0, :], func=ACT.Sin, bias=math.pi / 2)
        nc.scalar.activation(out=trig[:, 2, rest], in_=angle[:, rest], func=ACT.Sin)
        nc.scalar.activation(out=trig[:, 2, 0:WRAPPED], in_=wrapped[:, 1, :], func=ACT.Sin)
        bias_all = const.tile([P, OUT], F32)
        for h in range(HALVES):
            cols = slice(h * N_TILE, (h + 1) * N_TILE)
            spread = psum_acc.tile([P, N_TILE], F32, tag="acc")
            nc.tensor.matmul(spread[:], lhsT=ones[:], rhs=bias_rows[:, cols], start=True, stop=True)
            nc.scalar.copy(out=bias_all[:, cols], in_=spread[:])
        nc.scalar.activation(out=trig[:, 1, rest], in_=angle[:, rest], func=ACT.Sin, scale=-1.0)
        nc.scalar.activation(out=trig[:, 1, 0:WRAPPED], in_=wrapped[:, 1, :], func=ACT.Sin, scale=-1.0)

        orders = const.tile([P, 2, P], F32)
        nc.vector.tensor_single_scalar(orders[:], offsets[:], 0, op=ALU.is_equal)
        order_review = orders[:, 0, :]
        order_reply = orders[:, 1, :]
        w_planes = const.tile([P, OUT], U8, align_bytes=64)
        nc.vector.memset(w_planes[:].bitcast(I32), 0)
        reply_planes = const.tile([P, PASSES * MR * J * 2 * MQ], U8, align_bytes=64)
        nc.vector.memset(reply_planes[:].bitcast(I32), 0)
        for quadrant in range(4):
            nc.sync.dma_start(
                out=w_planes[32 * quadrant : 32 * quadrant + 16, :].bitcast(I32),
                in_=W_scales[:, 4 * quadrant : 4 * quadrant + 4, :].bitcast(I32),
            )
        for g in range(PASSES, 2 * PASSES):
            load_codes(g)
        for g in range(1, GROUPS):
            nc.sync.dma_start(out=x_review[g][:], in_=review_rows[g])
            nc.sync.dma_start(out=x_reply[g][:], in_=reply_rows[g])

        def rotary_products(x):
            engine = nc.gpsimd
            pairs = x[:].rearrange("p (i e) -> p i e", e=2)
            straight = work_g.tile([P, PAIRS, 2], F32, tag="straight")
            crossed = work_g.tile([P, 2, PAIRS], F32, tag="crossed")
            engine.tensor_tensor(
                out=straight[:], in0=pairs, in1=cos.unsqueeze(2).to_broadcast([P, PAIRS, 2]), op=ALU.mult
            )
            engine.tensor_tensor(out=crossed[:, 0, :], in0=pairs[:, :, 1], in1=minus_sin, op=ALU.mult)
            engine.tensor_tensor(out=crossed[:, 1, :], in0=pairs[:, :, 0], in1=sin, op=ALU.mult)
            return straight, crossed

        halves = [slice(g * PAIRS // PASSES, (g + 1) * PAIRS // PASSES) for g in range(PASSES)]

        def straight_product_vector(tiles, x, g):
            nc.vector.tensor_tensor(
                out=tiles[0][:, g * K_PASS : (g + 1) * K_PASS].rearrange("p (u e i) -> p u e i", u=2, e=2),
                in0=x[:, g * K_PASS : (g + 1) * K_PASS].rearrange("p (i u e) -> p u e i", u=2, e=2),
                in1=cos[:, halves[g]].rearrange("p (i u) -> p u i", u=2).unsqueeze(2).to_broadcast([P, 2, 2, P]),
                op=ALU.mult,
            )

        def crossed_products_vector(tiles, x, g):
            features = x[:, g * K_PASS : (g + 1) * K_PASS].rearrange("p (i u e) -> p e u i", u=2, e=2)
            sine = sin[:, halves[g]].rearrange("p (i u) -> p u i", u=2)
            planes = tiles[1][:, g].rearrange("p e (u i) -> p e u i", u=2)
            nc.vector.tensor_tensor(out=planes[:, 1], in0=features[:, 0], in1=sine, op=ALU.mult)
            nc.vector.scalar_tensor_tensor(
                out=planes[:, 0], in0=features[:, 1], scalar=-1.0, in1=sine, op0=ALU.mult, op1=ALU.mult
            )

        def product_tiles_vector():
            straight = work_v.tile([P, FEATURES], F32, tag="straight")
            crossed = work_v.tile([P, PASSES, 2, PAIRS // PASSES], F32, tag="crossed")
            return straight, crossed

        def keep_warm(products):
            nc.tensor.matmul(
                warm_bank[:, 0 : 2 * P], lhsT=order_review, rhs=products[0][:, 0 : 2 * P], start=True, stop=True
            )

        def transpose_planes(products, order, g, pool, tag):
            straight, crossed = products
            planes = pool.tile([P, PACK, P], F32, tag=tag)
            for t in range(PACK):
                u, e = t // 2, t % 2
                nc.tensor.matmul(
                    planes[:, t, :], lhsT=straight[:, K_PASS * g + t * P : K_PASS * g + (t + 1) * P], rhs=order,
                    is_transpose=True, start=True, stop=False,
                )
                nc.tensor.matmul(
                    planes[:, t, :], lhsT=crossed[:, g, e, u * P : (u + 1) * P], rhs=order,
                    is_transpose=True, start=False, stop=True,
                )
            return planes

        def transpose_sums(products, order, g):
            straight, crossed = products
            features = straight[:].rearrange("p i e -> p (i e)")
            planes = psum_t.tile([P, PACK, P], F32, tag="planes")
            for t in range(PACK):
                u, e = t // 2, t % 2
                nc.tensor.matmul(
                    planes[:, t, :], lhsT=features[:, K_PASS * g + t : K_PASS * (g + 1) : PACK], rhs=order,
                    is_transpose=True, start=True, stop=False,
                )
                nc.tensor.matmul(
                    planes[:, t, :], lhsT=crossed[:, e, 256 * g + u : 256 * (g + 1) : 2], rhs=order,
                    is_transpose=True, start=False, stop=True,
                )
            return planes

        def round_review(grouped, g, planes):
            nc.scalar.copy(
                out=grouped[:, g],
                in_=planes[:].rearrange("p t c -> p c t").unsqueeze(2).to_broadcast([P, P, MQ, PACK]),
            )

        def round_reply(grouped, g, planes):
            for twin in range(2):
                nc.scalar.copy(
                    out=grouped[:, :, g, :, twin, :, :],
                    in_=planes[:].rearrange("p t (d a q) -> p d a q t", d=PARTS, q=MQ),
                )

        def round_reply_part(grouped, g, planes, part):
            width = PART_MR * J * MQ
            nc.scalar.copy(
                out=grouped[:, part, g],
                in_=planes[:, :, part * width : (part + 1) * width]
                .rearrange("p t (a q) -> p a q t", q=MQ)
                .unsqueeze(2)
                .to_broadcast([P, PART_MR * J, 2, MQ, PACK]),
            )

        def quantize_review(grouped):
            review_codes = packed.tile([P, PASSES * NR * P], I32, tag="review_codes", align_bytes=64)
            review_planes = packed.tile([P, PASSES * NR * P], U8, tag="review_planes", align_bytes=64)
            nc.vector.quantize_mx(
                out=review_codes[:].bitcast(FP8X4),
                scales=review_planes[:],
                in_=grouped[:].rearrange("p g c r t -> p (g c r t)"),
            )
            return review_codes, review_planes

        PART_WORDS = PASSES * PART_MR * J * 2 * MQ

        def reply_tiles():
            reply_codes = packed.tile([P, PARTS * PART_WORDS], I32, tag="reply_codes", align_bytes=64)
            spread_codes = packed.tile([P, PARTS, PASSES, PART_MR, P], I32, tag="spread_codes", align_bytes=64)
            spread_planes = packed.tile([P, PARTS, PASSES, PART_MR, P], U8, tag="spread_planes", align_bytes=64)
            return reply_codes, spread_codes, spread_planes

        def quantize_reply(grouped, tiles, part):
            words = slice(part * PART_WORDS, (part + 1) * PART_WORDS)
            nc.vector.quantize_mx(
                out=tiles[0][:, words].bitcast(FP8X4),
                scales=reply_planes[:, words],
                in_=grouped[:, part].rearrange("p g a r q t -> p (g a r q t)"),
            )

        def spread_reply(tiles, part):
            reply_codes, spread_codes, spread_planes = tiles
            runs = PASSES * PART_MR * J
            nc.vector.tensor_copy(
                out=spread_codes[:, part].rearrange("p g r (j a w) -> p (g r j) a w", a=NQ // 2, w=2 * MQ),
                in_=reply_codes[:, part * PART_WORDS : (part + 1) * PART_WORDS]
                .rearrange("p (c w) -> p c w", w=2 * MQ)
                .unsqueeze(2)
                .to_broadcast([P, runs, NQ // 2, 2 * MQ]),
            )
            nc.vector.tensor_copy(
                out=spread_planes[:, part].bitcast(I32).rearrange("p g r (j a) -> p (g r j) a", a=NQ // 2),
                in_=reply_planes[:].bitcast(I32)[:, part * runs : (part + 1) * runs]
                .unsqueeze(2)
                .to_broadcast([P, runs, NQ // 2]),
            )

        def multiply(codes, planes, first_pass, h):
            cols = slice(h * N_TILE, (h + 1) * N_TILE)
            acc = psum_acc.tile([P, N_TILE], F32, tag="acc")
            for g in range(PASSES):
                nc.tensor.matmul_mx(
                    out=acc[:],
                    lhsT=codes[g].bitcast(FP8X4),
                    lhsT_scale=planes[g],
                    rhs=w_codes[:, first_pass + g, cols].bitcast(FP8X4),
                    rhs_scale=w_planes[4 * (first_pass + g) : P, cols],
                    start=(g == 0),
                    stop=(g == PASSES - 1),
                )
            return acc

        def multiply_review(operands, bank):
            nr, h = bank // HALVES, bank % HALVES
            review_codes, review_planes = operands
            blocks = [slice((g * NR + nr) * P, (g * NR + nr + 1) * P) for g in range(PASSES)]
            return multiply(
                [review_codes[:, block] for block in blocks], [review_planes[:, block] for block in blocks], 0, h
            )

        def multiply_reply(operands, bank):
            mr, h = bank // HALVES, bank % HALVES
            spread_codes, spread_planes = operands[1], operands[2]
            return multiply(
                [spread_codes[:, mr // PART_MR, g, mr % PART_MR, :] for g in range(PASSES)],
                [spread_planes[:, mr // PART_MR, g, mr % PART_MR, :] for g in range(PASSES)],
                PASSES,
                h,
            )

        def add_bias(review_sum, bank, acc):
            nr, h = bank // HALVES, bank % HALVES
            cols = slice(h * N_TILE, (h + 1) * N_TILE)
            nc.vector.tensor_tensor(out=review_sum[:, nr, cols], in0=acc[:], in1=bias_all[:, cols], op=ALU.add)

        gate = const.tile([P, 1], I32)

        def hold_gpsimd(spread_planes):
            nc.gpsimd.tensor_copy(out=gate[:], in_=spread_planes[:, PARTS - 1, 0, 0, 0:4].bitcast(I32))

        out_rows = out.rearrange(
            "(g j) (nq nr) (mq mr) o -> g nr (j nq) mq (mr o)", j=J, nr=NR, mq=MQ
        )
        BANKS = MR * HALVES
        REVIEW_BANKS = NR * HALVES
        y_review = [None] * GROUPS
        y_reply = [None] * GROUPS
        grouped_review = [None] * GROUPS
        grouped_reply = [None] * GROUPS
        review_operands = [None] * GROUPS
        reply_operands = [None] * GROUPS
        review_sums = [None] * GROUPS
        review_accs = {}
        reply_accs = {}

        def finish_preparation(group):
            review_sum = packed.tile([P, NR, OUT], F32, tag="review_sum")
            review_sums[group] = review_sum
            tiles = reply_tiles()
            reply_operands[group] = tiles
            order = (0, HALVES) if group == 0 else range(REVIEW_BANKS)
            quantize_reply(grouped_reply[group], tiles, 0)
            add_bias(review_sum, order[0], review_accs[(group, order[0])])
            spread_reply(tiles, 0)
            reply_accs[(group, 0)] = multiply_reply(tiles, 0)
            reply_accs[(group, 1)] = multiply_reply(tiles, 1)
            quantize_reply(grouped_reply[group], tiles, 1)
            add_bias(review_sum, order[1], review_accs[(group, order[1])])
            spread_reply(tiles, 1)
            if group + 1 < GROUPS:
                hold_gpsimd(tiles[2])
                y_review[group + 1] = rotary_products(x_review[group + 1])
                y_reply[group + 1] = rotary_products(x_reply[group + 1])
            for bank in order[2:]:
                add_bias(review_sum, bank, review_accs[(group, bank)])
            reply_accs[(group, 2)] = multiply_reply(tiles, 2)
            reply_accs[(group, 3)] = multiply_reply(tiles, 3)

        def table(group, steps):
            following = group + 1
            step_at = {}
            first = 0
            for step in steps:
                step_at[first] = step
                first += step
            stage = None
            first_mr = 0
            for bank in range(BANKS):
                mr, h = bank // HALVES, bank % HALVES
                cols = slice(h * N_TILE, (h + 1) * N_TILE)
                if group == 0 and bank == 1:
                    for review_bank in range(1, REVIEW_BANKS, HALVES):
                        add_bias(review_sums[0], review_bank, review_accs[(0, review_bank)])
                    reply_accs[(0, LEAD)] = multiply_reply(reply_operands[0], LEAD)
                if (group > 0 or bank > 0) and bank + LEAD < BANKS:
                    reply_accs[(group, bank + LEAD)] = multiply_reply(reply_operands[group], bank + LEAD)
                if following < GROUPS and bank > QUANTIZE_AT:
                    for review_bank in range(REVIEW_BANKS):
                        if min(QUANTIZE_AT + 1 + review_bank, BANKS - 1) == bank:
                            review_accs[(following, review_bank)] = multiply_review(
                                review_operands[following], review_bank
                            )
                if following < GROUPS and 0 <= bank - TURN_REVIEW_AT < PASSES:
                    planes_review = transpose_sums(y_review[following], order_review, bank - TURN_REVIEW_AT)
                if following < GROUPS and 0 <= bank - TURN_REPLY_AT < PASSES:
                    planes_reply = transpose_sums(y_reply[following], order_reply, bank - TURN_REPLY_AT)
                if h == 0 and mr in step_at:
                    stage = stages.tile([P, NR, MAX_STEP, OUT], F32, tag="stage")
                    first_mr = mr
                s = mr - first_mr
                if group == GROUPS - 1 and bank == BANKS - 1:
                    middle = h * N_TILE + N_TILE // 2
                    for nr in range(NR):
                        nc.vector.tensor_tensor(
                            out=stage[:, nr, s, cols],
                            in0=reply_accs[(group, bank)][:],
                            in1=review_sums[group][:, nr, cols],
                            op=ALU.add,
                        )
                        early, late = stage[:, nr, s, cols.start : middle], stage[:, nr, s, middle : cols.stop]
                        nc.scalar.activation(out=early, in_=early, func=ACT.Relu)
                        nc.gpsimd.tensor_scalar(
                            out=late, in0=late, scalar1=float("inf"), scalar2=0.0, op0=ALU.min, op1=ALU.max
                        )
                        nc.sync.dma_start(
                            out=out_rows[group, nr][:, :, mr * OUT + cols.start : mr * OUT + cols.stop],
                            in_=stage[:, nr, s, cols],
                        )
                    continue
                nc.vector.tensor_tensor(
                    out=stage[:, :, s, cols],
                    in0=reply_accs[(group, bank)][:].unsqueeze(1).to_broadcast([P, NR, N_TILE]),
                    in1=review_sums[group][:, :, cols],
                    op=ALU.add,
                )
                if (group == GROUPS - 1 and mr >= MR - 2) or (group == 0 and mr == 0):
                    if group == 0:
                        nc.scalar.activation(out=stage[:, :, s, cols], in_=stage[:, :, s, cols], func=ACT.Relu)
                    else:
                        nc.scalar.activation(out=stage[:, 0, s, cols], in_=stage[:, 0, s, cols], func=ACT.Relu)
                        nc.gpsimd.tensor_scalar(
                            out=stage[:, 1, s, cols], in0=stage[:, 1, s, cols],
                            scalar1=float("inf"), scalar2=0.0, op0=ALU.min, op1=ALU.max,
                        )
                    for nr in range(NR):
                        nc.sync.dma_start(
                            out=out_rows[group, nr][:, :, mr * OUT + cols.start : mr * OUT + cols.stop],
                            in_=stage[:, nr, s, cols],
                        )
                elif h == HALVES - 1:
                    if following == GROUPS:
                        nc.scalar.activation(out=stage[:, 0, s, :], in_=stage[:, 0, s, :], func=ACT.Relu)
                        nc.gpsimd.tensor_scalar(
                            out=stage[:, 1, s, :], in0=stage[:, 1, s, :],
                            scalar1=float("inf"), scalar2=0.0, op0=ALU.min, op1=ALU.max,
                        )
                    elif mr == GPSIMD_RELU:
                        nc.gpsimd.tensor_scalar(
                            out=stage[:, :, s, :], in0=stage[:, :, s, :],
                            scalar1=float("inf"), scalar2=0.0, op0=ALU.min, op1=ALU.max,
                        )
                    else:
                        nc.scalar.activation(out=stage[:, :, s, :], in_=stage[:, :, s, :], func=ACT.Relu)
                    if s == step_at[first_mr] - 1:
                        for nr in range(NR):
                            nc.sync.dma_start(
                                out=out_rows[group, nr][:, :, first_mr * OUT : (mr + 1) * OUT],
                                in_=stage[:, nr, 0 : s + 1, :].rearrange("p s o -> p (s o)"),
                            )
                if following < GROUPS and bank == TURN_REVIEW_AT:
                    rounded = grouped_pool.tile([P, PASSES, P, MQ, PACK], BF16, tag="grouped_review", align_bytes=64)
                    grouped_review[following] = rounded
                if following < GROUPS and 0 <= bank - TURN_REVIEW_AT < PASSES:
                    round_review(grouped_review[following], bank - TURN_REVIEW_AT, planes_review)
                if following < GROUPS and bank == TURN_REPLY_AT:
                    rounded = grouped_pool.tile(
                        [P, PARTS, PASSES, PART_MR * J, 2, MQ, PACK], BF16, tag="grouped_reply", align_bytes=64
                    )
                    grouped_reply[following] = rounded
                if following < GROUPS and 0 <= bank - TURN_REPLY_AT < PASSES:
                    round_reply(grouped_reply[following], bank - TURN_REPLY_AT, planes_reply)
                if following < GROUPS and bank == QUANTIZE_AT:
                    review_operands[following] = quantize_review(grouped_review[following])

        first_review = product_tiles_vector()
        first_reply = product_tiles_vector()
        for g in range(PASSES):
            straight_product_vector(first_review, x_review[0], g)
        for g in range(PASSES):
            crossed_products_vector(first_review, x_review[0], g)
        for g in range(PASSES):
            straight_product_vector(first_reply, x_reply[0], g)
            crossed_products_vector(first_reply, x_reply[0], g)
        rounded = grouped_pool.tile([P, PASSES, P, MQ, PACK], BF16, tag="grouped_review", align_bytes=64)
        keep_warm(first_review)
        for g in range(PASSES):
            round_review(rounded, g, transpose_planes(first_review, order_review, g, psum_t, "planes"))
        review_operands[0] = quantize_review(rounded)
        planes_reply = []
        for g in range(PASSES):
            keep_warm(first_review)
            planes_reply.append(transpose_planes(first_reply, order_reply, g, psum_acc, "acc"))
        rounded = grouped_pool.tile(
            [P, PARTS, PASSES, PART_MR * J, 2, MQ, PACK], BF16, tag="grouped_reply", align_bytes=64
        )
        grouped_reply[0] = rounded
        for part in range(PARTS):
            for g in range(PASSES):
                round_reply_part(rounded, g, planes_reply[g], part)
        for h in range(HALVES):
            for bank in range(h, REVIEW_BANKS, HALVES):
                review_accs[(0, bank)] = multiply_review(review_operands[0], bank)
        for group in range(GROUPS):
            finish_preparation(group)
            table(group, [1] * 8)
